import numpy as np
import ml_dtypes

BF16 = ml_dtypes.bfloat16


def bf(x):
    return np.asarray(x, np.float32).astype(BF16)


def f32(x):
    return np.asarray(x, np.float32)


def f64(x):
    return np.asarray(x).astype(np.float64)


def striped(idx):
    return np.tile(idx.reshape(-1, 16).T, (8, 1))


B, NN, H, E, MID, C, S, N = 8, 128, 128, 128, 128, 512, 2048, 1024
BIG = 1000000.0


def setup_inputs():
    return {
        "node_fts": bf(np.random.standard_normal((H, N))),
        "hidden": bf(np.random.standard_normal((H, N))),
        "edge_fts": bf(np.random.standard_normal((E, B, NN, NN))),
        "adj": bf(np.maximum(np.random.random((B, NN, NN)) < 0.5, np.eye(NN))),
        "graph_msg": f32(np.random.standard_normal((MID, B))),
        "W1": bf(np.random.standard_normal((H + H, MID)) / np.sqrt(H + H)),
        "b1": f32(0.1 * np.random.standard_normal((MID, 1))),
        "W2": bf(np.random.standard_normal((H + H, MID)) / np.sqrt(H + H)),
        "b2": f32(0.1 * np.random.standard_normal((MID, 1))),
        "We": bf(np.random.standard_normal((E, MID)) / np.sqrt(E)),
        "be": f32(0.1 * np.random.standard_normal((MID, 1))),
        "Wo1": bf(np.random.standard_normal((H + H, C)) / np.sqrt(H + H)),
        "bo1": f32(0.1 * np.random.standard_normal((C, 1))),
        "Wo2": bf(np.random.standard_normal((MID, C)) / np.sqrt(MID)),
        "bo2": f32(0.1 * np.random.standard_normal((C, 1))),
        "base": f32(np.random.standard_normal((C, S))),
        "offs": striped(np.random.permutation(S)[:N]),
    }


def reference(node_fts, hidden, edge_fts, adj, graph_msg, W1, b1, W2, b2, We, be, Wo1, bo1, Wo2, bo2, base, offs):
    idx = offs[:16].T.reshape(-1)
    z = np.concatenate([f64(node_fts), f64(hidden)], axis=0)
    m1 = f64(W1).T @ z + f64(b1)
    m2 = f64(W2).T @ z + f64(b2)
    msg = (f64(We).T @ f64(edge_fts).reshape(E, B * NN * NN) + f64(be)).reshape(MID, B, NN, NN)
    msg += m1.reshape(MID, B, NN, 1)
    msg += m2.reshape(MID, B, 1, NN)
    msg += f64(graph_msg).reshape(MID, B, 1, 1)
    red = np.where(f64(adj)[None] > 0, msg, -BIG).max(axis=3).reshape(MID, N)
    pre = (f64(Wo1).T @ z + f64(bo1)) + (f64(Wo2).T @ red + f64(bo2))
    pos = (pre > 0).astype(np.float64)
    out = f64(base).copy()
    out[:, idx] = pre * pos
    return out

@@ -1,0 +1,200 @@
+import concourse.mybir as mybir
+from concourse.masks import make_identity
+
+BF16, F32, U16 = mybir.dt.bfloat16, mybir.dt.float32, mybir.dt.uint16
+ALU = mybir.AluOpType
+FUNC = mybir.ActivationFunctionType
+INNERMOST = mybir.AxisListType.X
+
+P = 128
+GRAPHS = 8
+NODES = 128
+N = GRAPHS * NODES
+CHANNELS = 512
+CHANNEL_BLOCKS = CHANNELS // P
+SLOTS = 2048
+BANK = 512
+SENDERS = 32
+RANGES = NODES // SENDERS
+RECEIVERS = BANK // SENDERS
+PIECES = 3
+MASK_ROW = PIECES * SENDERS
+HALF_LIST = N // 2
+CHUNK = NODES // 2
+
+PENALTY = 2.0**100
+FLOOR = -1000000.0
+
+FLOPS = 2 * (P * P * GRAPHS * NODES * NODES + 2 * 2 * P * P * N + 2 * P * CHANNELS * N + P * CHANNELS * N)
+
+
+def tile_pgn_b_kernel(
+    tc, node_fts, hidden, edge_fts, adj, graph_msg, W1, b1, W2, b2, We, be, Wo1, bo1, Wo2, bo2, base, offs, out
+):
+    nc = tc.nc
+    with (
+        tc.tile_pool(name="held", bufs=1) as held,
+        tc.tile_pool(name="edges", bufs=4) as edges,
+        tc.tile_pool(name="work", bufs=2) as work,
+        tc.psum_pool(name="banks", bufs=6) as banks,
+        tc.psum_pool(name="side", bufs=2) as side,
+    ):
+        def load(shape, dtype, source, name):
+            tile = held.tile(shape, dtype, name=name)
+            nc.sync.dma_start(tile[:], source)
+            return tile
+
+        def load_edges(i):
+            t, c = divmod(i, NODES // CHUNK)
+            chunk = edges.tile([P, CHUNK, NODES], BF16)
+            nc.sync.dma_start(chunk[:], edge_fts[:, t, c * CHUNK : (c + 1) * CHUNK, :])
+            return chunk
+
+        node = load([P, N], BF16, node_fts, "node")
+        hid = load([P, N], BF16, hidden, "hid")
+        w2 = load([P, 2, P], BF16, W2.rearrange("(h k) m -> k h m", h=2), "w2")
+        adj_rows = held.tile([P, NODES, SENDERS], BF16)
+        for r in range(RANGES):
+            first = MASK_ROW + GRAPHS * r
+            nc.sync.dma_start(adj_rows[first : first + GRAPHS], adj[:, :, r * SENDERS : (r + 1) * SENDERS])
+        next_chunk = load_edges(0)
+        we = load([P, P], BF16, We, "we")
+        w1 = load([P, 2, P], BF16, W1.rearrange("(h k) m -> k h m", h=2), "w1")
+        graph_term = load([P, GRAPHS], F32, graph_msg, "graph_term")
+        b1_col = load([P, 1], F32, b1, "b1_col")
+        b2_col = load([P, 1], F32, b2, "b2_col")
+        be_col = load([P, 1], F32, be, "be_col")
+        offsets = held.tile([P, N // 16], U16, name="offsets")
+        nc.sync.dma_start(offsets[:], offs)
+        wo1 = load([P, 2, CHANNELS], BF16, Wo1.rearrange("(h k) c -> k h c", h=2), "wo1")
+        wo2 = load([P, CHANNELS], BF16, Wo2, "wo2")
+        with nc.allow_non_contiguous_dma(reason="two bias vectors of 512, one element to a partition"):
+            bo1_cols = load([P, CHANNEL_BLOCKS], F32, bo1.rearrange("(b c) one -> c (b one)", c=P), "bo1_cols")
+            bo2_cols = load([P, CHANNEL_BLOCKS], F32, bo2.rearrange("(b c) one -> c (b one)", c=P), "bo2_cols")
+
+        ident = held.tile([P, P], BF16)
+        make_identity(nc, ident[:])
+        same_sender = held.tile([P, SENDERS], F32)
+        nc.vector.tensor_reduce(
+            same_sender[:], ident[:].rearrange("p (s u) -> p u s", u=SENDERS), axis=INNERMOST, op=ALU.add
+        )
+        addend_rows = held.tile([P, NODES, SENDERS], BF16)
+        nc.vector.tensor_copy(
+            addend_rows[0:MASK_ROW],
+            same_sender[0:MASK_ROW].unsqueeze(1).to_broadcast([MASK_ROW, NODES, SENDERS]),
+        )
+        nc.vector.tensor_scalar(
+            addend_rows[MASK_ROW:P], adj_rows[MASK_ROW:P], 0.0, -PENALTY, op0=ALU.is_le, op1=ALU.mult
+        )
+
+        addend_weights = held.tile([P, RANGES, GRAPHS, P], BF16)
+        nc.gpsimd.tensor_copy(
+            addend_weights[MASK_ROW:P].rearrange("p r t m -> p (r t) m"),
+            ident[MASK_ROW:P, MASK_ROW:P].unsqueeze(2).to_broadcast([P - MASK_ROW, RANGES * GRAPHS, P]),
+        )
+
+        def times_z(weights, half):
+            cols = slice(half * BANK, (half + 1) * BANK)
+            product = side.tile([P, BANK], F32, tag="side")
+            nc.tensor.matmul(product[:], weights[:, 0, :], node[:, cols], start=True, stop=False)
+            nc.tensor.matmul(product[:], weights[:, 1, :], hid[:, cols], start=False, stop=True)
+            return product
+
+        sender_term = held.tile([P, N], F32)
+        for half in range(2):
+            nc.scalar.copy(sender_term[:, half * BANK : (half + 1) * BANK], times_z(w2, half)[:])
+
+        def make_addend_weights(t):
+            value = sender_term[:, t * NODES : (t + 1) * NODES].rearrange("p (r u) -> p r u", u=SENDERS)
+            pieces = work.tile([P, RANGES, PIECES, SENDERS], BF16)
+            high, middle, low = pieces[:, :, 0, :], pieces[:, :, 1, :], pieces[:, :, 2, :]
+            rest = work.tile([P, RANGES, SENDERS], F32)
+            nc.gpsimd.tensor_copy(high, value)
+            nc.gpsimd.tensor_sub(rest[:], value, high)
+            nc.gpsimd.tensor_copy(middle, rest[:])
+            nc.gpsimd.tensor_sub(low, rest[:], middle)
+            flipped = side.tile([MASK_ROW, RANGES, P], BF16, tag="side")
+            for r in range(RANGES):
+                nc.tensor.transpose(flipped[:, r, :], pieces[:, r, :, :].rearrange("p s u -> p (s u)"), ident[:])
+            nc.scalar.copy(addend_weights[0:MASK_ROW, :, t, :], flipped[:])
+
+        make_addend_weights(0)
+
+        bias_sum = held.tile([P, 1], F32)
+        nc.gpsimd.tensor_add(bias_sum[:], b1_col[:], b2_col[:])
+        nc.gpsimd.tensor_add(bias_sum[:], bias_sum[:], be_col[:])
+        graph_bias = held.tile([P, GRAPHS], F32)
+        nc.gpsimd.tensor_scalar_add(graph_bias[:], graph_term[:], bias_sum[:, 0:1])
+        receiver_term = held.tile([P, GRAPHS, NODES], F32)
+        for half in range(2):
+            product = times_z(w1, half)
+            for q in range(GRAPHS // 2):
+                t = half * (GRAPHS // 2) + q
+                nc.scalar.activation(
+                    receiver_term[:, t, :],
+                    product[:, q * NODES : (q + 1) * NODES],
+                    FUNC.Identity,
+                    bias=graph_bias[:, t : t + 1],
+                    scale=1.0,
+                )
+
+        candidates = held.tile([P, GRAPHS, RANGES + 1, NODES], F32)
+        nc.gpsimd.tensor_scalar(
+            candidates[:, :, RANGES, :], receiver_term[:], -1.0, FLOOR, op0=ALU.mult, op1=ALU.add
+        )
+
+        out_bias = held.tile([P, CHANNEL_BLOCKS], F32)
+        nc.gpsimd.tensor_add(out_bias[:], bo1_cols[:], bo2_cols[:])
+
+        red = held.tile([P, N], BF16)
+        slots = [held.tile([P, SLOTS], F32, name=f"slots{b}") for b in range(CHANNEL_BLOCKS)]
+
+        def place(half, b):
+            cols = slice(half * HALF_LIST, (half + 1) * HALF_LIST)
+            chans = slice(b * P, (b + 1) * P)
+            product = side.tile([P, HALF_LIST], F32, tag="side")
+            nc.tensor.matmul(product[:], wo1[:, 0, chans], node[:, cols], start=True, stop=False)
+            nc.tensor.matmul(product[:], wo1[:, 1, chans], hid[:, cols], start=False, stop=False)
+            nc.tensor.matmul(product[:], wo2[:, chans], red[:, cols], start=False, stop=True)
+            pre = work.tile([P, HALF_LIST], F32)
+            nc.scalar.activation(pre[:], product[:], FUNC.Identity, bias=out_bias[:, b : b + 1], scale=1.0)
+            pos = work.tile([P, HALF_LIST], F32)
+            nc.gpsimd.tensor_single_scalar(pos[:], pre[:], 0.0, op=ALU.is_gt)
+            piece = offsets[:, half * (HALF_LIST // 16) : (half + 1) * (HALF_LIST // 16)]
+            nc.vector.tensor_tensor(slots[b][:].indirect(piece), pre[:], pos[:], ALU.mult)
+
+        for t in range(GRAPHS):
+            for c in range(NODES // CHUNK):
+                i = t * (NODES // CHUNK) + c
+                chunk = next_chunk
+                if i + 1 < GRAPHS * (NODES // CHUNK):
+                    next_chunk = load_edges(i + 1)
+                if i < CHANNEL_BLOCKS:
+                    nc.sync.dma_start(slots[i][:], base[i * P : (i + 1) * P, :])
+
+                for g in range(CHUNK // RECEIVERS):
+                    here = slice(g * RECEIVERS, (g + 1) * RECEIVERS)
+                    group = c * (CHUNK // RECEIVERS) + g
+                    rows = slice(group * RECEIVERS, (group + 1) * RECEIVERS)
+                    for r in range(RANGES):
+                        bank = banks.tile([P, RECEIVERS, SENDERS], F32)
+                        nc.tensor.matmul(
+                            bank[:], we[:], chunk[:, here, r * SENDERS : (r + 1) * SENDERS], start=True, stop=False
+                        )
+                        nc.tensor.matmul(
+                            bank[:], addend_weights[:, r, t, :], addend_rows[:, rows, :], start=False, stop=True
+                        )
+                        nc.vector.reduce_max(candidates[:, t, r, rows], bank[:], axis=INNERMOST)
+                    if t == GRAPHS // 2 and group % 2 == 0:
+                        place(0, group // 2)
+
+                if c == 0 and t + 1 < GRAPHS:
+                    make_addend_weights(t + 1)
+
+            best = work.tile([P, NODES], F32)
+            nc.vector.reduce_max(best[:], candidates[:, t, :, :].rearrange("p s v -> p v s"), axis=INNERMOST)
+            nc.gpsimd.tensor_add(red[:, t * NODES : (t + 1) * NODES], best[:], receiver_term[:, t, :])
+
+        for b in range(CHANNEL_BLOCKS):
+            place(1, b)
+            nc.sync.dma_start(out[b * P : (b + 1) * P, :], slots[b][:])

@@ -21,6 +21,8 @@ PIECES = 3
 MASK_ROW = PIECES * SENDERS
 HALF_LIST = N // 2
 CHUNK = NODES // 2
+CHUNK_GROUPS = CHUNK // RECEIVERS
+REDUCED_WIDTH = 8
 
 PENALTY = 2.0**100
 FLOOR = -1000000.0
@@ -36,6 +38,7 @@ def tile_pgn_b_kernel(
         tc.tile_pool(name="held", bufs=1) as held,
         tc.tile_pool(name="edges", bufs=4) as edges,
         tc.tile_pool(name="work", bufs=2) as work,
+        tc.tile_pool(name="fresh", bufs=3) as fresh,
         tc.psum_pool(name="banks", bufs=6) as banks,
         tc.psum_pool(name="side", bufs=2) as side,
     ):
@@ -104,7 +107,7 @@ def tile_pgn_b_kernel(
         for half in range(2):
             nc.scalar.copy(sender_term[:, half * BANK : (half + 1) * BANK], times_z(w2, half)[:])
 
-        def make_addend_weights(t):
+        def cut_in_pieces(t):
             value = sender_term[:, t * NODES : (t + 1) * NODES].rearrange("p (r u) -> p r u", u=SENDERS)
             pieces = work.tile([P, RANGES, PIECES, SENDERS], BF16)
             high, middle, low = pieces[:, :, 0, :], pieces[:, :, 1, :], pieces[:, :, 2, :]
@@ -113,12 +116,18 @@ def tile_pgn_b_kernel(
             nc.gpsimd.tensor_sub(rest[:], value, high)
             nc.gpsimd.tensor_copy(middle, rest[:])
             nc.gpsimd.tensor_sub(low, rest[:], middle)
+            return pieces
+
+        def flip(pieces):
             flipped = side.tile([MASK_ROW, RANGES, P], BF16, tag="side")
             for r in range(RANGES):
                 nc.tensor.transpose(flipped[:, r, :], pieces[:, r, :, :].rearrange("p s u -> p (s u)"), ident[:])
+            return flipped
+
+        def keep(flipped, t):
             nc.scalar.copy(addend_weights[0:MASK_ROW, :, t, :], flipped[:])
 
-        make_addend_weights(0)
+        keep(flip(cut_in_pieces(0)), 0)
 
         bias_sum = held.tile([P, 1], F32)
         nc.gpsimd.tensor_add(bias_sum[:], b1_col[:], b2_col[:])
@@ -172,28 +181,65 @@ def tile_pgn_b_kernel(
                 if i < CHANNEL_BLOCKS:
                     nc.sync.dma_start(slots[i][:], base[i * P : (i + 1) * P, :])
 
-                for g in range(CHUNK // RECEIVERS):
-                    here = slice(g * RECEIVERS, (g + 1) * RECEIVERS)
-                    group = c * (CHUNK // RECEIVERS) + g
-                    rows = slice(group * RECEIVERS, (group + 1) * RECEIVERS)
-                    for r in range(RANGES):
+                for r in range(RANGES):
+                    senders = slice(r * SENDERS, (r + 1) * SENDERS)
+                    for g in range(CHUNK_GROUPS):
+                        here = slice(g * RECEIVERS, (g + 1) * RECEIVERS)
+                        first = c * CHUNK + g * RECEIVERS
+                        rows = slice(first, first + RECEIVERS)
                         bank = banks.tile([P, RECEIVERS, SENDERS], F32)
-                        nc.tensor.matmul(
-                            bank[:], we[:], chunk[:, here, r * SENDERS : (r + 1) * SENDERS], start=True, stop=False
-                        )
+                        nc.tensor.matmul(bank[:], we[:], chunk[:, here, senders], start=True, stop=False)
                         nc.tensor.matmul(
                             bank[:], addend_weights[:, r, t, :], addend_rows[:, rows, :], start=False, stop=True
                         )
-                        nc.vector.reduce_max(candidates[:, t, r, rows], bank[:], axis=INNERMOST)
-                    if t == GRAPHS // 2 and group % 2 == 0:
-                        place(0, group // 2)
+                        if g == 0:
+                            rounded = fresh.tile([P, RECEIVERS, SENDERS], BF16)
+                            for v in range(RECEIVERS):
+                                nc.scalar.activation(
+                                    rounded[:, v, :],
+                                    bank[:, v, :],
+                                    FUNC.Identity,
+                                    bias=receiver_term[:, t, first + v : first + v + 1],
+                                    scale=1.0,
+                                )
+                        else:
+                            nc.vector.reduce_max(candidates[:, t, r, rows], bank[:], axis=INNERMOST)
+                    if r == 0:
+                        best = rounded
+                    else:
+                        better = work.tile([P, RECEIVERS, SENDERS], BF16)
+                        nc.vector.tensor_max(better[:], best[:], rounded[:])
+                        best = better
 
-                if c == 0 and t + 1 < GRAPHS:
-                    make_addend_weights(t + 1)
+                    if c == 0 and t + 1 < GRAPHS:
+                        if r == 0:
+                            pieces = cut_in_pieces(t + 1)
+                        if r == 2:
+                            flipped = flip(pieces)
+                        if r == 3:
+                            keep(flipped, t + 1)
+                    if t == GRAPHS // 2 and r % 2 == 0:
+                        place(0, c * (RANGES // 2) + r // 2)
 
-            best = work.tile([P, NODES], F32)
-            nc.vector.reduce_max(best[:], candidates[:, t, :, :].rearrange("p s v -> p v s"), axis=INNERMOST)
-            nc.gpsimd.tensor_add(red[:, t * NODES : (t + 1) * NODES], best[:], receiver_term[:, t, :])
+                start = t * NODES + c * CHUNK
+                wide = best
+                for width in (SENDERS // 2, SENDERS // 4):
+                    narrow = work.tile([P, RECEIVERS, width], BF16, name=f"narrow{width}")
+                    nc.vector.tensor_max(narrow[:], wide[:, :, 0:width], wide[:, :, width : 2 * width])
+                    wide = narrow
+                with nc.allow_low_precision(reason="a max picks one of its inputs: nothing is accumulated"):
+                    nc.vector.reduce_max(red[:, start : start + RECEIVERS], wide[:], axis=INNERMOST)
+                nc.vector.tensor_scalar_max(
+                    red[:, start : start + RECEIVERS], red[:, start : start + RECEIVERS], FLOOR
+                )
+                others = slice(c * CHUNK + RECEIVERS, (c + 1) * CHUNK)
+                winner = work.tile([P, CHUNK - RECEIVERS], F32)
+                nc.vector.reduce_max(
+                    winner[:], candidates[:, t, :, others].rearrange("p s v -> p v s"), axis=INNERMOST
+                )
+                nc.gpsimd.tensor_add(
+                    red[:, start + RECEIVERS : start + CHUNK], winner[:], receiver_term[:, t, others]
+                )
 
         for b in range(CHANNEL_BLOCKS):
             place(1, b)

@@ -14,15 +14,20 @@ CHANNELS = 512
 CHANNEL_BLOCKS = CHANNELS // P
 SLOTS = 2048
 BANK = 512
+BANK_RECEIVERS = BANK // NODES
 SENDERS = 32
 RANGES = NODES // SENDERS
-RECEIVERS = BANK // SENDERS
 PIECES = 3
 MASK_ROW = PIECES * SENDERS
-HALF_LIST = N // 2
 CHUNK = NODES // 2
-CHUNK_GROUPS = CHUNK // RECEIVERS
+CHUNKS = GRAPHS * NODES // CHUNK
+TURN = 4
+GROUP_TURNS = 2
+GROUPS = CHUNK // (BANK_RECEIVERS * TURN * GROUP_TURNS)
+SCALAR_RECEIVERS = (TURN - 1) * GROUP_TURNS * BANK_RECEIVERS
+VECTOR_RECEIVERS = GROUP_TURNS * BANK_RECEIVERS
 REDUCED_WIDTH = 8
+PLACED = 2 * NODES
 
 PENALTY = 2.0**100
 FLOOR = -1000000.0
@@ -134,23 +139,18 @@ def tile_pgn_b_kernel(
         nc.gpsimd.tensor_add(bias_sum[:], bias_sum[:], be_col[:])
         graph_bias = held.tile([P, GRAPHS], F32)
         nc.gpsimd.tensor_scalar_add(graph_bias[:], graph_term[:], bias_sum[:, 0:1])
-        receiver_term = held.tile([P, GRAPHS, NODES], F32)
+        receiver_term = held.tile([P, N], F32)
         for half in range(2):
             product = times_z(w1, half)
             for q in range(GRAPHS // 2):
                 t = half * (GRAPHS // 2) + q
                 nc.scalar.activation(
-                    receiver_term[:, t, :],
+                    receiver_term[:, t * NODES : (t + 1) * NODES],
                     product[:, q * NODES : (q + 1) * NODES],
                     FUNC.Identity,
                     bias=graph_bias[:, t : t + 1],
                     scale=1.0,
                 )
-
-        candidates = held.tile([P, GRAPHS, RANGES + 1, NODES], F32)
-        nc.gpsimd.tensor_scalar(
-            candidates[:, :, RANGES, :], receiver_term[:], -1.0, FLOOR, op0=ALU.mult, op1=ALU.add
-        )
 
         out_bias = held.tile([P, CHANNEL_BLOCKS], F32)
         nc.gpsimd.tensor_add(out_bias[:], bo1_cols[:], bo2_cols[:])
@@ -158,89 +158,112 @@ def tile_pgn_b_kernel(
         red = held.tile([P, N], BF16)
         slots = [held.tile([P, SLOTS], F32, name=f"slots{b}") for b in range(CHANNEL_BLOCKS)]
 
-        def place(half, b):
-            cols = slice(half * HALF_LIST, (half + 1) * HALF_LIST)
+        def fill_bank(chunk, t, node_0, within):
+            bank = banks.tile([P, BANK_RECEIVERS, NODES], F32)
+            nc.tensor.matmul(bank[:], we[:], chunk[:, within : within + BANK_RECEIVERS, :], start=True, stop=False)
+            v = node_0 - t * NODES
+            for r in range(RANGES):
+                nc.tensor.matmul(
+                    bank[:, :, r * SENDERS : (r + 1) * SENDERS],
+                    addend_weights[:, r, t, :],
+                    addend_rows[:, v : v + BANK_RECEIVERS, :],
+                    start=False,
+                    stop=(r == RANGES - 1),
+                )
+            return bank
+
+        def fold(wide, width):
+            narrow = work.tile([P, SCALAR_RECEIVERS, width], BF16, name=f"narrow{width}")
+            nc.vector.tensor_max(narrow[:], wide[:, :, 0:width], wide[:, :, width : 2 * width])
+            return narrow
+
+        def fold_to_the_end(wide, width, node_0):
+            while width > REDUCED_WIDTH:
+                width //= 2
+                wide = fold(wide, width)
+            with nc.allow_low_precision(reason="a max picks one of its inputs: nothing is accumulated"):
+                nc.vector.reduce_max(red[:, node_0 : node_0 + SCALAR_RECEIVERS], wide[:], axis=INNERMOST)
+
+        def prepare(k, b):
+            cols = slice(k * PLACED, (k + 1) * PLACED)
             chans = slice(b * P, (b + 1) * P)
-            product = side.tile([P, HALF_LIST], F32, tag="side")
+            if b == 0:
+                nc.vector.tensor_scalar_max(red[:, cols], red[:, cols], FLOOR)
+            product = side.tile([P, PLACED], F32, tag="side")
             nc.tensor.matmul(product[:], wo1[:, 0, chans], node[:, cols], start=True, stop=False)
             nc.tensor.matmul(product[:], wo1[:, 1, chans], hid[:, cols], start=False, stop=False)
             nc.tensor.matmul(product[:], wo2[:, chans], red[:, cols], start=False, stop=True)
-            pre = work.tile([P, HALF_LIST], F32)
+            pre = work.tile([P, PLACED], F32)
             nc.scalar.activation(pre[:], product[:], FUNC.Identity, bias=out_bias[:, b : b + 1], scale=1.0)
-            pos = work.tile([P, HALF_LIST], F32)
+            pos = work.tile([P, PLACED], F32)
             nc.gpsimd.tensor_single_scalar(pos[:], pre[:], 0.0, op=ALU.is_gt)
-            piece = offsets[:, half * (HALF_LIST // 16) : (half + 1) * (HALF_LIST // 16)]
+            return pre, pos
+
+        def place(k, b, pre, pos):
+            piece = offsets[:, k * (PLACED // 16) : (k + 1) * (PLACED // 16)]
             nc.vector.tensor_tensor(slots[b][:].indirect(piece), pre[:], pos[:], ALU.mult)
 
-        for t in range(GRAPHS):
-            for c in range(NODES // CHUNK):
-                i = t * (NODES // CHUNK) + c
-                chunk = next_chunk
-                if i + 1 < GRAPHS * (NODES // CHUNK):
-                    next_chunk = load_edges(i + 1)
-                if i < CHANNEL_BLOCKS:
-                    nc.sync.dma_start(slots[i][:], base[i * P : (i + 1) * P, :])
+        unfolded = None
+        for i in range(CHUNKS):
+            t, c = divmod(i, NODES // CHUNK)
+            chunk = next_chunk
+            if i + 1 < CHUNKS:
+                next_chunk = load_edges(i + 1)
+            if i < CHANNEL_BLOCKS:
+                nc.sync.dma_start(slots[i][:], base[i * P : (i + 1) * P, :])
+            k, b = divmod(i, CHANNEL_BLOCKS)
 
-                for r in range(RANGES):
-                    senders = slice(r * SENDERS, (r + 1) * SENDERS)
-                    for g in range(CHUNK_GROUPS):
-                        here = slice(g * RECEIVERS, (g + 1) * RECEIVERS)
-                        first = c * CHUNK + g * RECEIVERS
-                        rows = slice(first, first + RECEIVERS)
-                        bank = banks.tile([P, RECEIVERS, SENDERS], F32)
-                        nc.tensor.matmul(bank[:], we[:], chunk[:, here, senders], start=True, stop=False)
-                        nc.tensor.matmul(
-                            bank[:], addend_weights[:, r, t, :], addend_rows[:, rows, :], start=False, stop=True
-                        )
-                        if g == 0:
-                            rounded = fresh.tile([P, RECEIVERS, SENDERS], BF16)
-                            for v in range(RECEIVERS):
-                                nc.scalar.activation(
-                                    rounded[:, v, :],
-                                    bank[:, v, :],
-                                    FUNC.Identity,
-                                    bias=receiver_term[:, t, first + v : first + v + 1],
-                                    scale=1.0,
-                                )
-                        else:
-                            nc.vector.reduce_max(candidates[:, t, r, rows], bank[:], axis=INNERMOST)
-                    if r == 0:
-                        best = rounded
+            for g in range(GROUPS):
+                scalar_0 = g * SCALAR_RECEIVERS
+                vector_0 = GROUPS * SCALAR_RECEIVERS + g * VECTOR_RECEIVERS
+                rounded = fresh.tile([P, SCALAR_RECEIVERS, NODES], BF16)
+                winners = fresh.tile([P, VECTOR_RECEIVERS], F32)
+                for turn in range(GROUP_TURNS):
+                    for s in range(turn * (TURN - 1), (turn + 1) * (TURN - 1)):
+                        within = scalar_0 + s * BANK_RECEIVERS
+                        node_0 = i * CHUNK + within
+                        bank = fill_bank(chunk, t, node_0, within)
+                        for v in range(BANK_RECEIVERS):
+                            nc.scalar.activation(
+                                rounded[:, s * BANK_RECEIVERS + v, :],
+                                bank[:, v, :],
+                                FUNC.Identity,
+                                bias=receiver_term[:, node_0 + v : node_0 + v + 1],
+                                scale=1.0,
+                            )
+                    within = vector_0 + turn * BANK_RECEIVERS
+                    bank = fill_bank(chunk, t, i * CHUNK + within, within)
+                    nc.vector.reduce_max(
+                        winners[:, turn * BANK_RECEIVERS : (turn + 1) * BANK_RECEIVERS], bank[:], axis=INNERMOST
+                    )
+
+                    if turn == 0:
+                        if unfolded is not None:
+                            quarter = fold(fold(unfolded[0], NODES // 2), NODES // 4)
+                        if c == 0 and t + 1 < GRAPHS:
+                            if g == 0:
+                                pieces = cut_in_pieces(t + 1)
+                            else:
+                                flipped = flip(pieces)
+                        if k > 0 and g == GROUPS - 1:
+                            pre, pos = prepare(k - 1, b)
                     else:
-                        better = work.tile([P, RECEIVERS, SENDERS], BF16)
-                        nc.vector.tensor_max(better[:], best[:], rounded[:])
-                        best = better
-
-                    if c == 0 and t + 1 < GRAPHS:
-                        if r == 0:
-                            pieces = cut_in_pieces(t + 1)
-                        if r == 2:
-                            flipped = flip(pieces)
-                        if r == 3:
+                        if unfolded is not None:
+                            fold_to_the_end(quarter, NODES // 4, unfolded[1])
+                        unfolded = (rounded, i * CHUNK + scalar_0)
+                        won = slice(i * CHUNK + vector_0, i * CHUNK + vector_0 + VECTOR_RECEIVERS)
+                        nc.vector.tensor_add(red[:, won], winners[:], receiver_term[:, won])
+                        if c == 0 and t + 1 < GRAPHS and g == GROUPS - 1:
                             keep(flipped, t + 1)
-                    if t == GRAPHS // 2 and r % 2 == 0:
-                        place(0, c * (RANGES // 2) + r // 2)
+                        if k > 0 and g == GROUPS - 1:
+                            place(k - 1, b, pre, pos)
 
-                start = t * NODES + c * CHUNK
-                wide = best
-                for width in (SENDERS // 2, SENDERS // 4):
-                    narrow = work.tile([P, RECEIVERS, width], BF16, name=f"narrow{width}")
-                    nc.vector.tensor_max(narrow[:], wide[:, :, 0:width], wide[:, :, width : 2 * width])
-                    wide = narrow
-                with nc.allow_low_precision(reason="a max picks one of its inputs: nothing is accumulated"):
-                    nc.vector.reduce_max(red[:, start : start + RECEIVERS], wide[:], axis=INNERMOST)
-                nc.vector.tensor_scalar_max(
-                    red[:, start : start + RECEIVERS], red[:, start : start + RECEIVERS], FLOOR
-                )
-                others = slice(c * CHUNK + RECEIVERS, (c + 1) * CHUNK)
-                winner = work.tile([P, CHUNK - RECEIVERS], F32)
-                nc.vector.reduce_max(
-                    winner[:], candidates[:, t, :, others].rearrange("p s v -> p v s"), axis=INNERMOST
-                )
-                nc.gpsimd.tensor_add(
-                    red[:, start + RECEIVERS : start + CHUNK], winner[:], receiver_term[:, t, others]
-                )
-
+        fold_to_the_end(unfolded[0], NODES, unfolded[1])
+        last = N // PLACED - 1
+        ready = prepare(last, 0)
         for b in range(CHANNEL_BLOCKS):
-            place(1, b)
+            pre, pos = ready
+            if b + 1 < CHANNEL_BLOCKS:
+                ready = prepare(last, b + 1)
+            place(last, b, pre, pos)
             nc.sync.dma_start(out[b * P : (b + 1) * P, :], slots[b][:])

@@ -19,15 +19,17 @@ SENDERS = 32
 RANGES = NODES // SENDERS
 PIECES = 3
 MASK_ROW = PIECES * SENDERS
-CHUNK = NODES // 2
-CHUNKS = GRAPHS * NODES // CHUNK
+CHUNK = NODES // 4
+CHUNKS = N // CHUNK
+GRAPH_CHUNKS = NODES // CHUNK
 TURN = 4
-GROUP_TURNS = 2
-GROUPS = CHUNK // (BANK_RECEIVERS * TURN * GROUP_TURNS)
-SCALAR_RECEIVERS = (TURN - 1) * GROUP_TURNS * BANK_RECEIVERS
-VECTOR_RECEIVERS = GROUP_TURNS * BANK_RECEIVERS
+TURNS = CHUNK // (BANK_RECEIVERS * TURN)
+SCALAR_RECEIVERS = (TURN - 1) * TURNS * BANK_RECEIVERS
+VECTOR_RECEIVERS = TURNS * BANK_RECEIVERS
 REDUCED_WIDTH = 8
 PLACED = 2 * NODES
+LOADS_AHEAD = 2
+FIRST_PLACING_CHUNK = PLACED // CHUNK + 1
 
 PENALTY = 2.0**100
 FLOOR = -1000000.0
@@ -41,7 +43,7 @@ def tile_pgn_b_kernel(
     nc = tc.nc
     with (
         tc.tile_pool(name="held", bufs=1) as held,
-        tc.tile_pool(name="edges", bufs=4) as edges,
+        tc.tile_pool(name="edges", bufs=6) as edges,
         tc.tile_pool(name="work", bufs=2) as work,
         tc.tile_pool(name="fresh", bufs=3) as fresh,
         tc.psum_pool(name="banks", bufs=6) as banks,
@@ -53,7 +55,7 @@ def tile_pgn_b_kernel(
             return tile
 
         def load_edges(i):
-            t, c = divmod(i, NODES // CHUNK)
+            t, c = divmod(i, GRAPH_CHUNKS)
             chunk = edges.tile([P, CHUNK, NODES], BF16)
             nc.sync.dma_start(chunk[:], edge_fts[:, t, c * CHUNK : (c + 1) * CHUNK, :])
             return chunk
@@ -65,13 +67,15 @@ def tile_pgn_b_kernel(
         for r in range(RANGES):
             first = MASK_ROW + GRAPHS * r
             nc.sync.dma_start(adj_rows[first : first + GRAPHS], adj[:, :, r * SENDERS : (r + 1) * SENDERS])
-        next_chunk = load_edges(0)
         we = load([P, P], BF16, We, "we")
+        loaded = [load_edges(0)]
         w1 = load([P, 2, P], BF16, W1.rearrange("(h k) m -> k h m", h=2), "w1")
         graph_term = load([P, GRAPHS], F32, graph_msg, "graph_term")
         b1_col = load([P, 1], F32, b1, "b1_col")
         b2_col = load([P, 1], F32, b2, "b2_col")
         be_col = load([P, 1], F32, be, "be_col")
+        for i in range(1, LOADS_AHEAD):
+            loaded.append(load_edges(i))
         offsets = held.tile([P, N // 16], U16, name="offsets")
         nc.sync.dma_start(offsets[:], offs)
         wo1 = load([P, 2, CHANNELS], BF16, Wo1.rearrange("(h k) c -> k h c", h=2), "wo1")
@@ -82,45 +86,68 @@ def tile_pgn_b_kernel(
 
         ident = held.tile([P, P], BF16)
         make_identity(nc, ident[:])
-        same_sender = held.tile([P, SENDERS], F32)
-        nc.vector.tensor_reduce(
-            same_sender[:], ident[:].rearrange("p (s u) -> p u s", u=SENDERS), axis=INNERMOST, op=ALU.add
-        )
+        same_sender = held.tile([P, SENDERS], BF16)
+        with nc.allow_low_precision(reason="each sum is of zeros and at most a single 1"):
+            nc.vector.tensor_reduce(
+                same_sender[:], ident[:].rearrange("p (s u) -> p u s", u=SENDERS), axis=INNERMOST, op=ALU.add
+            )
         addend_rows = held.tile([P, NODES, SENDERS], BF16)
-        nc.vector.tensor_copy(
-            addend_rows[0:MASK_ROW],
-            same_sender[0:MASK_ROW].unsqueeze(1).to_broadcast([MASK_ROW, NODES, SENDERS]),
-        )
-        nc.vector.tensor_scalar(
-            addend_rows[MASK_ROW:P], adj_rows[MASK_ROW:P], 0.0, -PENALTY, op0=ALU.is_le, op1=ALU.mult
-        )
+
+        def write_addend_rows(c):
+            rows = slice(c * CHUNK, (c + 1) * CHUNK)
+            nc.vector.tensor_copy(
+                addend_rows[0:MASK_ROW, rows, :],
+                same_sender[0:MASK_ROW].unsqueeze(1).to_broadcast([MASK_ROW, CHUNK, SENDERS]),
+            )
+            nc.vector.tensor_scalar(
+                addend_rows[MASK_ROW:P, rows, :], adj_rows[MASK_ROW:P, rows, :], 0.0, -PENALTY, op0=ALU.is_le, op1=ALU.mult
+            )
 
         addend_weights = held.tile([P, RANGES, GRAPHS, P], BF16)
-        nc.gpsimd.tensor_copy(
-            addend_weights[MASK_ROW:P].rearrange("p r t m -> p (r t) m"),
-            ident[MASK_ROW:P, MASK_ROW:P].unsqueeze(2).to_broadcast([P - MASK_ROW, RANGES * GRAPHS, P]),
-        )
+        picks = ident[MASK_ROW:P, MASK_ROW:P].rearrange("p (r t) -> p r t", t=GRAPHS)
+        for t in range(GRAPHS):
+            nc.gpsimd.tensor_scalar(
+                addend_weights[MASK_ROW:P, :, t, :],
+                picks[:, :, t].unsqueeze(2).to_broadcast([P - MASK_ROW, RANGES, P]),
+                1.0,
+                0.0,
+                op0=ALU.mult,
+                op1=ALU.add,
+            )
 
-        def times_z(weights, half):
-            cols = slice(half * BANK, (half + 1) * BANK)
-            product = side.tile([P, BANK], F32, tag="side")
-            nc.tensor.matmul(product[:], weights[:, 0, :], node[:, cols], start=True, stop=False)
-            nc.tensor.matmul(product[:], weights[:, 1, :], hid[:, cols], start=False, stop=True)
-            return product
+        bias_sum = held.tile([P, 1], F32)
+        nc.gpsimd.tensor_add(bias_sum[:], b1_col[:], b2_col[:])
+        nc.gpsimd.tensor_add(bias_sum[:], bias_sum[:], be_col[:])
+        graph_bias = held.tile([P, GRAPHS], F32)
+        nc.gpsimd.tensor_scalar_add(graph_bias[:], graph_term[:], bias_sum[:, 0:1])
+        receiver_term = held.tile([P, N], F32)
 
-        sender_term = held.tile([P, N], F32)
-        for half in range(2):
-            nc.scalar.copy(sender_term[:, half * BANK : (half + 1) * BANK], times_z(w2, half)[:])
+        def multiply_by_z(t):
+            cols = slice(t * NODES, (t + 1) * NODES)
+            products = []
+            for weights in (w2, w1):
+                product = side.tile([P, NODES], F32, tag="side")
+                nc.tensor.matmul(product[:], weights[:, 0, :], node[:, cols], start=True, stop=False)
+                nc.tensor.matmul(product[:], weights[:, 1, :], hid[:, cols], start=False, stop=True)
+                products.append(product)
+            return products
 
-        def cut_in_pieces(t):
-            value = sender_term[:, t * NODES : (t + 1) * NODES].rearrange("p (r u) -> p r u", u=SENDERS)
+        def take_terms(products, t):
+            nc.scalar.activation(
+                receiver_term[:, t * NODES : (t + 1) * NODES],
+                products[1][:],
+                FUNC.Identity,
+                bias=graph_bias[:, t : t + 1],
+                scale=1.0,
+            )
+            value = products[0][:].rearrange("p (r u) -> p r u", u=SENDERS)
             pieces = work.tile([P, RANGES, PIECES, SENDERS], BF16)
             high, middle, low = pieces[:, :, 0, :], pieces[:, :, 1, :], pieces[:, :, 2, :]
             rest = work.tile([P, RANGES, SENDERS], F32)
-            nc.gpsimd.tensor_copy(high, value)
-            nc.gpsimd.tensor_sub(rest[:], value, high)
-            nc.gpsimd.tensor_copy(middle, rest[:])
-            nc.gpsimd.tensor_sub(low, rest[:], middle)
+            nc.vector.tensor_copy(high, value)
+            nc.vector.tensor_sub(rest[:], value, high)
+            nc.vector.tensor_copy(middle, rest[:])
+            nc.vector.tensor_sub(low, rest[:], middle)
             return pieces
 
         def flip(pieces):
@@ -132,25 +159,10 @@ def tile_pgn_b_kernel(
         def keep(flipped, t):
             nc.scalar.copy(addend_weights[0:MASK_ROW, :, t, :], flipped[:])
 
-        keep(flip(cut_in_pieces(0)), 0)
-
-        bias_sum = held.tile([P, 1], F32)
-        nc.gpsimd.tensor_add(bias_sum[:], b1_col[:], b2_col[:])
-        nc.gpsimd.tensor_add(bias_sum[:], bias_sum[:], be_col[:])
-        graph_bias = held.tile([P, GRAPHS], F32)
-        nc.gpsimd.tensor_scalar_add(graph_bias[:], graph_term[:], bias_sum[:, 0:1])
-        receiver_term = held.tile([P, N], F32)
-        for half in range(2):
-            product = times_z(w1, half)
-            for q in range(GRAPHS // 2):
-                t = half * (GRAPHS // 2) + q
-                nc.scalar.activation(
-                    receiver_term[:, t * NODES : (t + 1) * NODES],
-                    product[:, q * NODES : (q + 1) * NODES],
-                    FUNC.Identity,
-                    bias=graph_bias[:, t : t + 1],
-                    scale=1.0,
-                )
+        write_addend_rows(0)
+        keep(flip(take_terms(multiply_by_z(0), 0)), 0)
+        for c in range(1, GRAPH_CHUNKS):
+            write_addend_rows(c)
 
         out_bias = held.tile([P, CHANNEL_BLOCKS], F32)
         nc.gpsimd.tensor_add(out_bias[:], bo1_cols[:], bo2_cols[:])
@@ -184,11 +196,13 @@ def tile_pgn_b_kernel(
             with nc.allow_low_precision(reason="a max picks one of its inputs: nothing is accumulated"):
                 nc.vector.reduce_max(red[:, node_0 : node_0 + SCALAR_RECEIVERS], wide[:], axis=INNERMOST)
 
+        def lay_floor(k):
+            cols = slice(k * PLACED, (k + 1) * PLACED)
+            nc.vector.tensor_scalar_max(red[:, cols], red[:, cols], FLOOR)
+
         def prepare(k, b):
             cols = slice(k * PLACED, (k + 1) * PLACED)
             chans = slice(b * P, (b + 1) * P)
-            if b == 0:
-                nc.vector.tensor_scalar_max(red[:, cols], red[:, cols], FLOOR)
             product = side.tile([P, PLACED], F32, tag="side")
             nc.tensor.matmul(product[:], wo1[:, 0, chans], node[:, cols], start=True, stop=False)
             nc.tensor.matmul(product[:], wo1[:, 1, chans], hid[:, cols], start=False, stop=False)
@@ -203,67 +217,74 @@ def tile_pgn_b_kernel(
             piece = offsets[:, k * (PLACED // 16) : (k + 1) * (PLACED // 16)]
             nc.vector.tensor_tensor(slots[b][:].indirect(piece), pre[:], pos[:], ALU.mult)
 
+        placings = [(k, b) for k in range(N // PLACED) for b in range(CHANNEL_BLOCKS)]
         unfolded = None
         for i in range(CHUNKS):
-            t, c = divmod(i, NODES // CHUNK)
-            chunk = next_chunk
-            if i + 1 < CHUNKS:
-                next_chunk = load_edges(i + 1)
-            if i < CHANNEL_BLOCKS:
-                nc.sync.dma_start(slots[i][:], base[i * P : (i + 1) * P, :])
-            k, b = divmod(i, CHANNEL_BLOCKS)
+            t, c = divmod(i, GRAPH_CHUNKS)
+            chunk = loaded[i]
+            if i + LOADS_AHEAD < CHUNKS:
+                loaded.append(load_edges(i + LOADS_AHEAD))
+            if i % 2 == 1 and i // 2 < CHANNEL_BLOCKS:
+                nc.sync.dma_start(slots[i // 2][:], base[(i // 2) * P : (i // 2 + 1) * P, :])
+            places = i >= FIRST_PLACING_CHUNK and (i - FIRST_PLACING_CHUNK) % 2 == 0
+            makes_terms = t + 1 < GRAPHS
 
-            for g in range(GROUPS):
-                scalar_0 = g * SCALAR_RECEIVERS
-                vector_0 = GROUPS * SCALAR_RECEIVERS + g * VECTOR_RECEIVERS
-                rounded = fresh.tile([P, SCALAR_RECEIVERS, NODES], BF16)
-                winners = fresh.tile([P, VECTOR_RECEIVERS], F32)
-                for turn in range(GROUP_TURNS):
-                    for s in range(turn * (TURN - 1), (turn + 1) * (TURN - 1)):
-                        within = scalar_0 + s * BANK_RECEIVERS
-                        node_0 = i * CHUNK + within
-                        bank = fill_bank(chunk, t, node_0, within)
-                        for v in range(BANK_RECEIVERS):
-                            nc.scalar.activation(
-                                rounded[:, s * BANK_RECEIVERS + v, :],
-                                bank[:, v, :],
-                                FUNC.Identity,
-                                bias=receiver_term[:, node_0 + v : node_0 + v + 1],
-                                scale=1.0,
-                            )
-                    within = vector_0 + turn * BANK_RECEIVERS
-                    bank = fill_bank(chunk, t, i * CHUNK + within, within)
-                    nc.vector.reduce_max(
-                        winners[:, turn * BANK_RECEIVERS : (turn + 1) * BANK_RECEIVERS], bank[:], axis=INNERMOST
-                    )
+            rounded = fresh.tile([P, SCALAR_RECEIVERS, NODES], BF16)
+            winners = fresh.tile([P, VECTOR_RECEIVERS], F32)
+            for turn in range(TURNS):
+                for s in range(turn * (TURN - 1), (turn + 1) * (TURN - 1)):
+                    within = s * BANK_RECEIVERS
+                    node_0 = i * CHUNK + within
+                    bank = fill_bank(chunk, t, node_0, within)
+                    for v in range(BANK_RECEIVERS):
+                        nc.scalar.activation(
+                            rounded[:, within + v, :],
+                            bank[:, v, :],
+                            FUNC.Identity,
+                            bias=receiver_term[:, node_0 + v : node_0 + v + 1],
+                            scale=1.0,
+                        )
+                within = SCALAR_RECEIVERS + turn * BANK_RECEIVERS
+                bank = fill_bank(chunk, t, i * CHUNK + within, within)
+                nc.vector.reduce_max(
+                    winners[:, turn * BANK_RECEIVERS : (turn + 1) * BANK_RECEIVERS], bank[:], axis=INNERMOST
+                )
 
-                    if turn == 0:
-                        if unfolded is not None:
-                            quarter = fold(fold(unfolded[0], NODES // 2), NODES // 4)
-                        if c == 0 and t + 1 < GRAPHS:
-                            if g == 0:
-                                pieces = cut_in_pieces(t + 1)
-                            else:
-                                flipped = flip(pieces)
-                        if k > 0 and g == GROUPS - 1:
-                            pre, pos = prepare(k - 1, b)
-                    else:
-                        if unfolded is not None:
-                            fold_to_the_end(quarter, NODES // 4, unfolded[1])
-                        unfolded = (rounded, i * CHUNK + scalar_0)
-                        won = slice(i * CHUNK + vector_0, i * CHUNK + vector_0 + VECTOR_RECEIVERS)
-                        nc.vector.tensor_add(red[:, won], winners[:], receiver_term[:, won])
-                        if c == 0 and t + 1 < GRAPHS and g == GROUPS - 1:
-                            keep(flipped, t + 1)
-                        if k > 0 and g == GROUPS - 1:
-                            place(k - 1, b, pre, pos)
+                if turn == 0:
+                    if unfolded is not None:
+                        quarter = fold(fold(unfolded[0], NODES // 2), NODES // 4)
+                    if makes_terms and c == 0:
+                        products = multiply_by_z(t + 1)
+                    if makes_terms and c == 1:
+                        flipped = flip(pieces)
+                    if places:
+                        k, b = placings[(i - FIRST_PLACING_CHUNK) // 2]
+                        pre, pos = prepare(k, b)
+                else:
+                    if unfolded is not None:
+                        fold_to_the_end(quarter, NODES // 4, unfolded[1])
+                        if (i * CHUNK) % PLACED == 0:
+                            lay_floor(i * CHUNK // PLACED - 1)
+                    unfolded = (rounded, i * CHUNK)
+                    won = slice(i * CHUNK + SCALAR_RECEIVERS, (i + 1) * CHUNK)
+                    nc.vector.tensor_add(red[:, won], winners[:], receiver_term[:, won])
+                    if makes_terms and c == 0:
+                        pieces = take_terms(products, t + 1)
+                    if makes_terms and c == 1:
+                        keep(flipped, t + 1)
+                    if places:
+                        place(k, b, pre, pos)
 
         fold_to_the_end(unfolded[0], NODES, unfolded[1])
         last = N // PLACED - 1
-        ready = prepare(last, 0)
-        for b in range(CHANNEL_BLOCKS):
+        lay_floor(last)
+        left = placings[(CHUNKS - FIRST_PLACING_CHUNK + 1) // 2 :]
+        ready = prepare(left[0][0], left[0][1])
+        for n in range(len(left)):
+            k, b = left[n]
             pre, pos = ready
-            if b + 1 < CHANNEL_BLOCKS:
-                ready = prepare(last, b + 1)
-            place(last, b, pre, pos)
-            nc.sync.dma_start(out[b * P : (b + 1) * P, :], slots[b][:])
+            if n + 1 < len(left):
+                ready = prepare(left[n + 1][0], left[n + 1][1])
+            place(k, b, pre, pos)
+            if k == last:
+                nc.sync.dma_start(out[b * P : (b + 1) * P, :], slots[b][:])

@@ -210,7 +210,7 @@ def tile_pgn_b_kernel(
             pre = work.tile([P, PLACED], F32)
             nc.scalar.activation(pre[:], product[:], FUNC.Identity, bias=out_bias[:, b : b + 1], scale=1.0)
             pos = work.tile([P, PLACED], F32)
-            nc.gpsimd.tensor_single_scalar(pos[:], pre[:], 0.0, op=ALU.is_gt)
+            nc.vector.tensor_single_scalar(pos[:], pre[:], 0.0, op=ALU.is_gt)
             return pre, pos
 
         def place(k, b, pre, pos):

@@ -22,14 +22,14 @@ MASK_ROW = PIECES * SENDERS
 CHUNK = NODES // 4
 CHUNKS = N // CHUNK
 GRAPH_CHUNKS = NODES // CHUNK
+HEAD = CHUNK // 4
 TURN = 4
 TURNS = CHUNK // (BANK_RECEIVERS * TURN)
-SCALAR_RECEIVERS = (TURN - 1) * TURNS * BANK_RECEIVERS
-VECTOR_RECEIVERS = TURNS * BANK_RECEIVERS
+TURN_RECEIVERS = (TURN - 1) * BANK_RECEIVERS
 REDUCED_WIDTH = 8
 PLACED = 2 * NODES
-LOADS_AHEAD = 2
-FIRST_PLACING_CHUNK = PLACED // CHUNK + 1
+LOADS_AHEAD = 4
+GROUP_CHUNKS = PLACED // CHUNK
 
 PENALTY = 2.0**100
 FLOOR = -1000000.0
@@ -54,28 +54,37 @@ def tile_pgn_b_kernel(
             nc.sync.dma_start(tile[:], source)
             return tile
 
+        def load_part(tile, part, source):
+            nc.sync.dma_start(tile[:, part], source[:, part])
+
         def load_edges(i):
             t, c = divmod(i, GRAPH_CHUNKS)
             chunk = edges.tile([P, CHUNK, NODES], BF16)
             nc.sync.dma_start(chunk[:], edge_fts[:, t, c * CHUNK : (c + 1) * CHUNK, :])
             return chunk
 
-        node = load([P, N], BF16, node_fts, "node")
-        hid = load([P, N], BF16, hidden, "hid")
+        first_nodes, other_nodes = slice(0, 2 * NODES), slice(2 * NODES, N)
+        node = held.tile([P, N], BF16)
+        hid = held.tile([P, N], BF16)
+        load_part(node, first_nodes, node_fts)
+        load_part(hid, first_nodes, hidden)
         w2 = load([P, 2, P], BF16, W2.rearrange("(h k) m -> k h m", h=2), "w2")
-        adj_rows = held.tile([P, NODES, SENDERS], BF16)
-        for r in range(RANGES):
-            first = MASK_ROW + GRAPHS * r
-            nc.sync.dma_start(adj_rows[first : first + GRAPHS], adj[:, :, r * SENDERS : (r + 1) * SENDERS])
-        we = load([P, P], BF16, We, "we")
-        loaded = [load_edges(0)]
         w1 = load([P, 2, P], BF16, W1.rearrange("(h k) m -> k h m", h=2), "w1")
         graph_term = load([P, GRAPHS], F32, graph_msg, "graph_term")
         b1_col = load([P, 1], F32, b1, "b1_col")
         b2_col = load([P, 1], F32, b2, "b2_col")
         be_col = load([P, 1], F32, be, "be_col")
+        adj_rows = held.tile([P, CHUNK, NODES], BF16)
+        nc.sync.dma_start(adj_rows[MASK_ROW:P], adj.rearrange("t (c v) u -> (t c) v u", v=CHUNK))
+        we = load([P, P], BF16, We, "we")
+        first_edges = edge_fts[:, 0, 0:CHUNK, :]
+        loaded = [edges.tile([P, CHUNK, NODES], BF16, name="chunk")]
+        load_part(loaded[0], slice(0, HEAD), first_edges)
+        load_part(loaded[0], slice(HEAD, CHUNK), first_edges)
         for i in range(1, LOADS_AHEAD):
             loaded.append(load_edges(i))
+        load_part(node, other_nodes, node_fts)
+        load_part(hid, other_nodes, hidden)
         offsets = held.tile([P, N // 16], U16, name="offsets")
         nc.sync.dma_start(offsets[:], offs)
         wo1 = load([P, 2, CHANNELS], BF16, Wo1.rearrange("(h k) c -> k h c", h=2), "wo1")
@@ -91,35 +100,42 @@ def tile_pgn_b_kernel(
             nc.vector.tensor_reduce(
                 same_sender[:], ident[:].rearrange("p (s u) -> p u s", u=SENDERS), axis=INNERMOST, op=ALU.add
             )
-        addend_rows = held.tile([P, NODES, SENDERS], BF16)
+        pattern = held.tile([P, RANGES, SENDERS], BF16)
+        nc.vector.tensor_copy(pattern[:], same_sender[:].unsqueeze(1).to_broadcast([P, RANGES, SENDERS]))
+        addend_rows = held.tile([P, CHUNK, NODES], BF16)
 
-        def write_addend_rows(c):
-            rows = slice(c * CHUNK, (c + 1) * CHUNK)
+        def write_addend_rows(part):
+            size = part.stop - part.start
             nc.vector.tensor_copy(
-                addend_rows[0:MASK_ROW, rows, :],
-                same_sender[0:MASK_ROW].unsqueeze(1).to_broadcast([MASK_ROW, CHUNK, SENDERS]),
+                addend_rows[0:MASK_ROW, part, :],
+                pattern[0:MASK_ROW].rearrange("p r u -> p (r u)").unsqueeze(1).to_broadcast([MASK_ROW, size, NODES]),
             )
             nc.vector.tensor_scalar(
-                addend_rows[MASK_ROW:P, rows, :], adj_rows[MASK_ROW:P, rows, :], 0.0, -PENALTY, op0=ALU.is_le, op1=ALU.mult
+                addend_rows[MASK_ROW:P, part, :], adj_rows[MASK_ROW:P, part, :], 0.0, -PENALTY, op0=ALU.is_le, op1=ALU.mult
             )
 
-        addend_weights = held.tile([P, RANGES, GRAPHS, P], BF16)
-        picks = ident[MASK_ROW:P, MASK_ROW:P].rearrange("p (r t) -> p r t", t=GRAPHS)
-        for t in range(GRAPHS):
+        addend_weights = held.tile([P, GRAPHS, GRAPH_CHUNKS, RANGES, P], BF16)
+
+        def write_picks(t):
+            first = MASK_ROW + t * GRAPH_CHUNKS
             nc.gpsimd.tensor_scalar(
-                addend_weights[MASK_ROW:P, :, t, :],
-                picks[:, :, t].unsqueeze(2).to_broadcast([P - MASK_ROW, RANGES, P]),
+                addend_weights[MASK_ROW:P, t].rearrange("p c r m -> p c (r m)"),
+                ident[MASK_ROW:P, first : first + GRAPH_CHUNKS].unsqueeze(2).to_broadcast([P - MASK_ROW, GRAPH_CHUNKS, RANGES * P]),
                 1.0,
                 0.0,
                 op0=ALU.mult,
                 op1=ALU.add,
             )
 
-        bias_sum = held.tile([P, 1], F32)
-        nc.gpsimd.tensor_add(bias_sum[:], b1_col[:], b2_col[:])
-        nc.gpsimd.tensor_add(bias_sum[:], bias_sum[:], be_col[:])
-        graph_bias = held.tile([P, GRAPHS], F32)
-        nc.gpsimd.tensor_scalar_add(graph_bias[:], graph_term[:], bias_sum[:, 0:1])
+        write_picks(0)
+
+        graph_bias = graph_term
+        for name, bias in (("with_b1", b1_col), ("with_b2", b2_col), ("with_be", be_col)):
+            summed = held.tile([P, GRAPHS], F32, name=name)
+            nc.scalar.activation(summed[:], graph_bias[:], FUNC.Identity, bias=bias[:, 0:1], scale=1.0)
+            graph_bias = summed
+        for t in range(1, GRAPHS):
+            write_picks(t)
         receiver_term = held.tile([P, N], F32)
 
         def multiply_by_z(t):
@@ -157,12 +173,19 @@ def tile_pgn_b_kernel(
             return flipped
 
         def keep(flipped, t):
-            nc.scalar.copy(addend_weights[0:MASK_ROW, :, t, :], flipped[:])
+            nc.scalar.copy(addend_weights[0:MASK_ROW, t, 0], flipped[:])
 
-        write_addend_rows(0)
+        def repeat(t):
+            nc.sync.dma_start(
+                addend_weights[0:MASK_ROW, t, 1:GRAPH_CHUNKS],
+                addend_weights[0:MASK_ROW, t, 0:1].to_broadcast([MASK_ROW, GRAPH_CHUNKS - 1, RANGES, P]),
+            )
+
+        write_addend_rows(slice(0, HEAD))
         keep(flip(take_terms(multiply_by_z(0), 0)), 0)
+        write_addend_rows(slice(HEAD, CHUNK))
         for c in range(1, GRAPH_CHUNKS):
-            write_addend_rows(c)
+            nc.vector.tensor_copy(addend_weights[0:MASK_ROW, 0, c], addend_weights[0:MASK_ROW, 0, 0])
 
         out_bias = held.tile([P, CHANNEL_BLOCKS], F32)
         nc.gpsimd.tensor_add(out_bias[:], bo1_cols[:], bo2_cols[:])
@@ -170,31 +193,30 @@ def tile_pgn_b_kernel(
         red = held.tile([P, N], BF16)
         slots = [held.tile([P, SLOTS], F32, name=f"slots{b}") for b in range(CHANNEL_BLOCKS)]
 
-        def fill_bank(chunk, t, node_0, within):
+        def fill_bank(chunk, t, c, within):
             bank = banks.tile([P, BANK_RECEIVERS, NODES], F32)
             nc.tensor.matmul(bank[:], we[:], chunk[:, within : within + BANK_RECEIVERS, :], start=True, stop=False)
-            v = node_0 - t * NODES
             for r in range(RANGES):
                 nc.tensor.matmul(
                     bank[:, :, r * SENDERS : (r + 1) * SENDERS],
-                    addend_weights[:, r, t, :],
-                    addend_rows[:, v : v + BANK_RECEIVERS, :],
+                    addend_weights[:, t, c, r, :],
+                    addend_rows[:, within : within + BANK_RECEIVERS, r * SENDERS : (r + 1) * SENDERS],
                     start=False,
                     stop=(r == RANGES - 1),
                 )
             return bank
 
         def fold(wide, width):
-            narrow = work.tile([P, SCALAR_RECEIVERS, width], BF16, name=f"narrow{width}")
+            narrow = work.tile([P, wide.shape[1], width], BF16, name=f"narrow{width}")
             nc.vector.tensor_max(narrow[:], wide[:, :, 0:width], wide[:, :, width : 2 * width])
-            return narrow
+            return narrow[:]
 
         def fold_to_the_end(wide, width, node_0):
             while width > REDUCED_WIDTH:
                 width //= 2
                 wide = fold(wide, width)
             with nc.allow_low_precision(reason="a max picks one of its inputs: nothing is accumulated"):
-                nc.vector.reduce_max(red[:, node_0 : node_0 + SCALAR_RECEIVERS], wide[:], axis=INNERMOST)
+                nc.vector.reduce_max(red[:, node_0 : node_0 + wide.shape[1]], wide, axis=INNERMOST)
 
         def lay_floor(k):
             cols = slice(k * PLACED, (k + 1) * PLACED)
@@ -217,7 +239,6 @@ def tile_pgn_b_kernel(
             piece = offsets[:, k * (PLACED // 16) : (k + 1) * (PLACED // 16)]
             nc.vector.tensor_tensor(slots[b][:].indirect(piece), pre[:], pos[:], ALU.mult)
 
-        placings = [(k, b) for k in range(N // PLACED) for b in range(CHANNEL_BLOCKS)]
         unfolded = None
         for i in range(CHUNKS):
             t, c = divmod(i, GRAPH_CHUNKS)
@@ -226,29 +247,35 @@ def tile_pgn_b_kernel(
                 loaded.append(load_edges(i + LOADS_AHEAD))
             if i % 2 == 1 and i // 2 < CHANNEL_BLOCKS:
                 nc.sync.dma_start(slots[i // 2][:], base[(i // 2) * P : (i // 2 + 1) * P, :])
-            places = i >= FIRST_PLACING_CHUNK and (i - FIRST_PLACING_CHUNK) % 2 == 0
+            k, in_group = i // GROUP_CHUNKS - 1, i % GROUP_CHUNKS
+            places = k >= 0 and 1 <= in_group <= CHANNEL_BLOCKS
             makes_terms = t + 1 < GRAPHS
 
-            rounded = fresh.tile([P, SCALAR_RECEIVERS, NODES], BF16)
-            winners = fresh.tile([P, VECTOR_RECEIVERS], F32)
+            last_chunk = i + 1 == CHUNKS
+            scalar_turns = TURNS - 1 if last_chunk else TURNS
+            scalar_receivers = scalar_turns * TURN_RECEIVERS
+            rounded = fresh.tile([P, scalar_receivers, NODES], BF16)
+            winners = fresh.tile([P, CHUNK - scalar_receivers], F32)
+            scalar_next, vector_next = 0, scalar_receivers
             for turn in range(TURNS):
-                for s in range(turn * (TURN - 1), (turn + 1) * (TURN - 1)):
-                    within = s * BANK_RECEIVERS
-                    node_0 = i * CHUNK + within
-                    bank = fill_bank(chunk, t, node_0, within)
-                    for v in range(BANK_RECEIVERS):
-                        nc.scalar.activation(
-                            rounded[:, within + v, :],
-                            bank[:, v, :],
-                            FUNC.Identity,
-                            bias=receiver_term[:, node_0 + v : node_0 + v + 1],
-                            scale=1.0,
-                        )
-                within = SCALAR_RECEIVERS + turn * BANK_RECEIVERS
-                bank = fill_bank(chunk, t, i * CHUNK + within, within)
-                nc.vector.reduce_max(
-                    winners[:, turn * BANK_RECEIVERS : (turn + 1) * BANK_RECEIVERS], bank[:], axis=INNERMOST
-                )
+                for s in range(TURN):
+                    if turn < scalar_turns and s + 1 < TURN:
+                        bank = fill_bank(chunk, t, c, scalar_next)
+                        for v in range(BANK_RECEIVERS):
+                            receiver = i * CHUNK + scalar_next + v
+                            nc.scalar.activation(
+                                rounded[:, scalar_next + v, :],
+                                bank[:, v, :],
+                                FUNC.Identity,
+                                bias=receiver_term[:, receiver : receiver + 1],
+                                scale=1.0,
+                            )
+                        scalar_next += BANK_RECEIVERS
+                    else:
+                        bank = fill_bank(chunk, t, c, vector_next)
+                        won = vector_next - scalar_receivers
+                        nc.vector.reduce_max(winners[:, won : won + BANK_RECEIVERS], bank[:], axis=INNERMOST)
+                        vector_next += BANK_RECEIVERS
 
                 if turn == 0:
                     if unfolded is not None:
@@ -258,33 +285,33 @@ def tile_pgn_b_kernel(
                     if makes_terms and c == 1:
                         flipped = flip(pieces)
                     if places:
-                        k, b = placings[(i - FIRST_PLACING_CHUNK) // 2]
+                        b = in_group - 1
                         pre, pos = prepare(k, b)
-                else:
-                    if unfolded is not None:
+                    if last_chunk:
                         fold_to_the_end(quarter, NODES // 4, unfolded[1])
-                        if (i * CHUNK) % PLACED == 0:
-                            lay_floor(i * CHUNK // PLACED - 1)
-                    unfolded = (rounded, i * CHUNK)
-                    won = slice(i * CHUNK + SCALAR_RECEIVERS, (i + 1) * CHUNK)
-                    nc.vector.tensor_add(red[:, won], winners[:], receiver_term[:, won])
+                        fold_to_the_end(rounded[:], NODES, i * CHUNK)
+                else:
+                    if unfolded is not None and not last_chunk:
+                        fold_to_the_end(quarter, NODES // 4, unfolded[1])
+                    if k >= 0 and in_group == 0:
+                        lay_floor(k)
+                    unfolded = (rounded[:], i * CHUNK)
+                    nodes = slice(i * CHUNK + scalar_receivers, (i + 1) * CHUNK)
+                    nc.vector.tensor_add(red[:, nodes], winners[:], receiver_term[:, nodes])
                     if makes_terms and c == 0:
                         pieces = take_terms(products, t + 1)
                     if makes_terms and c == 1:
                         keep(flipped, t + 1)
+                        repeat(t + 1)
                     if places:
                         place(k, b, pre, pos)
 
-        fold_to_the_end(unfolded[0], NODES, unfolded[1])
         last = N // PLACED - 1
         lay_floor(last)
-        left = placings[(CHUNKS - FIRST_PLACING_CHUNK + 1) // 2 :]
-        ready = prepare(left[0][0], left[0][1])
-        for n in range(len(left)):
-            k, b = left[n]
+        ready = prepare(last, 0)
+        for b in range(CHANNEL_BLOCKS):
             pre, pos = ready
-            if n + 1 < len(left):
-                ready = prepare(left[n + 1][0], left[n + 1][1])
-            place(k, b, pre, pos)
-            if k == last:
-                nc.sync.dma_start(out[b * P : (b + 1) * P, :], slots[b][:])
+            if b + 1 < CHANNEL_BLOCKS:
+                ready = prepare(last, b + 1)
+            place(last, b, pre, pos)
+            nc.sync.dma_start(out[b * P : (b + 1) * P, :], slots[b][:])

@@ -1,7 +1,7 @@
 import concourse.mybir as mybir
 from concourse.masks import make_identity
 
-BF16, F32, U16 = mybir.dt.bfloat16, mybir.dt.float32, mybir.dt.uint16
+BF16, F32, I32, U16 = mybir.dt.bfloat16, mybir.dt.float32, mybir.dt.int32, mybir.dt.uint16
 ALU = mybir.AluOpType
 FUNC = mybir.ActivationFunctionType
 INNERMOST = mybir.AxisListType.X
@@ -25,11 +25,11 @@ GRAPH_CHUNKS = NODES // CHUNK
 HEAD = CHUNK // 4
 TURN = 4
 TURNS = CHUNK // (BANK_RECEIVERS * TURN)
-TURN_RECEIVERS = (TURN - 1) * BANK_RECEIVERS
 REDUCED_WIDTH = 8
 PLACED = 2 * NODES
 LOADS_AHEAD = 4
 GROUP_CHUNKS = PLACED // CHUNK
+PLACING_CHUNKS = (1, 3, 5, 6)
 
 PENALTY = 2.0**100
 FLOOR = -1000000.0
@@ -63,7 +63,7 @@ def tile_pgn_b_kernel(
             nc.sync.dma_start(chunk[:], edge_fts[:, t, c * CHUNK : (c + 1) * CHUNK, :])
             return chunk
 
-        first_nodes, other_nodes = slice(0, 2 * NODES), slice(2 * NODES, N)
+        first_nodes, other_nodes = slice(0, NODES), slice(NODES, N)
         node = held.tile([P, N], BF16)
         hid = held.tile([P, N], BF16)
         load_part(node, first_nodes, node_fts)
@@ -81,10 +81,11 @@ def tile_pgn_b_kernel(
         loaded = [edges.tile([P, CHUNK, NODES], BF16, name="chunk")]
         load_part(loaded[0], slice(0, HEAD), first_edges)
         load_part(loaded[0], slice(HEAD, CHUNK), first_edges)
-        for i in range(1, LOADS_AHEAD):
-            loaded.append(load_edges(i))
+        loaded.append(load_edges(1))
         load_part(node, other_nodes, node_fts)
         load_part(hid, other_nodes, hidden)
+        for i in range(2, LOADS_AHEAD):
+            loaded.append(load_edges(i))
         offsets = held.tile([P, N // 16], U16, name="offsets")
         nc.sync.dma_start(offsets[:], offs)
         wo1 = load([P, 2, CHANNELS], BF16, Wo1.rearrange("(h k) c -> k h c", h=2), "wo1")
@@ -100,31 +101,32 @@ def tile_pgn_b_kernel(
             nc.vector.tensor_reduce(
                 same_sender[:], ident[:].rearrange("p (s u) -> p u s", u=SENDERS), axis=INNERMOST, op=ALU.add
             )
-        pattern = held.tile([P, RANGES, SENDERS], BF16)
-        nc.vector.tensor_copy(pattern[:], same_sender[:].unsqueeze(1).to_broadcast([P, RANGES, SENDERS]))
-        addend_rows = held.tile([P, CHUNK, NODES], BF16)
+        addend_rows = held.tile([P, RANGES, CHUNK, SENDERS], BF16)
 
         def write_addend_rows(part):
             size = part.stop - part.start
             nc.vector.tensor_copy(
-                addend_rows[0:MASK_ROW, part, :],
-                pattern[0:MASK_ROW].rearrange("p r u -> p (r u)").unsqueeze(1).to_broadcast([MASK_ROW, size, NODES]),
+                addend_rows[0:MASK_ROW, :, part, :],
+                same_sender[0:MASK_ROW].unsqueeze(1).unsqueeze(1).to_broadcast([MASK_ROW, RANGES, size, SENDERS]),
             )
             nc.vector.tensor_scalar(
-                addend_rows[MASK_ROW:P, part, :], adj_rows[MASK_ROW:P, part, :], 0.0, -PENALTY, op0=ALU.is_le, op1=ALU.mult
+                addend_rows[MASK_ROW:P, :, part, :].rearrange("p r v u -> p v r u"),
+                adj_rows[MASK_ROW:P, part, :].rearrange("p v (r u) -> p v r u", u=SENDERS),
+                0.0,
+                -PENALTY,
+                op0=ALU.is_le,
+                op1=ALU.mult,
             )
 
         addend_weights = held.tile([P, GRAPHS, GRAPH_CHUNKS, RANGES, P], BF16)
+        pairs = held.tile([P, CHUNKS, 2], BF16)
+        nc.gpsimd.tensor_copy(pairs[MASK_ROW:P], ident[MASK_ROW:P, MASK_ROW:P].unsqueeze(2).to_broadcast([CHUNKS, CHUNKS, 2]))
 
         def write_picks(t):
-            first = MASK_ROW + t * GRAPH_CHUNKS
-            nc.gpsimd.tensor_scalar(
-                addend_weights[MASK_ROW:P, t].rearrange("p c r m -> p c (r m)"),
-                ident[MASK_ROW:P, first : first + GRAPH_CHUNKS].unsqueeze(2).to_broadcast([P - MASK_ROW, GRAPH_CHUNKS, RANGES * P]),
-                1.0,
-                0.0,
-                op0=ALU.mult,
-                op1=ALU.add,
+            chunks = slice(t * GRAPH_CHUNKS, (t + 1) * GRAPH_CHUNKS)
+            nc.gpsimd.tensor_copy(
+                addend_weights[MASK_ROW:P, t].rearrange("p c r m -> p c (r m)").bitcast(I32),
+                pairs[MASK_ROW:P, chunks].bitcast(I32).to_broadcast([CHUNKS, GRAPH_CHUNKS, RANGES * P // 2]),
             )
 
         write_picks(0)
@@ -200,7 +202,7 @@ def tile_pgn_b_kernel(
                 nc.tensor.matmul(
                     bank[:, :, r * SENDERS : (r + 1) * SENDERS],
                     addend_weights[:, t, c, r, :],
-                    addend_rows[:, within : within + BANK_RECEIVERS, r * SENDERS : (r + 1) * SENDERS],
+                    addend_rows[:, r, within : within + BANK_RECEIVERS, :],
                     start=False,
                     stop=(r == RANGES - 1),
                 )
@@ -248,18 +250,22 @@ def tile_pgn_b_kernel(
             if i % 2 == 1 and i // 2 < CHANNEL_BLOCKS:
                 nc.sync.dma_start(slots[i // 2][:], base[(i // 2) * P : (i // 2 + 1) * P, :])
             k, in_group = i // GROUP_CHUNKS - 1, i % GROUP_CHUNKS
-            places = k >= 0 and 1 <= in_group <= CHANNEL_BLOCKS
+            places = k >= 0 and in_group in PLACING_CHUNKS
             makes_terms = t + 1 < GRAPHS
 
             last_chunk = i + 1 == CHUNKS
-            scalar_turns = TURNS - 1 if last_chunk else TURNS
-            scalar_receivers = scalar_turns * TURN_RECEIVERS
+            scalar_banks = [TURN - 1] * TURNS
+            if places:
+                scalar_banks[-1] = TURN
+            if last_chunk:
+                scalar_banks[-1] = 0
+            scalar_receivers = sum(scalar_banks) * BANK_RECEIVERS
             rounded = fresh.tile([P, scalar_receivers, NODES], BF16)
             winners = fresh.tile([P, CHUNK - scalar_receivers], F32)
             scalar_next, vector_next = 0, scalar_receivers
             for turn in range(TURNS):
                 for s in range(TURN):
-                    if turn < scalar_turns and s + 1 < TURN:
+                    if s < scalar_banks[turn]:
                         bank = fill_bank(chunk, t, c, scalar_next)
                         for v in range(BANK_RECEIVERS):
                             receiver = i * CHUNK + scalar_next + v
@@ -285,7 +291,7 @@ def tile_pgn_b_kernel(
                     if makes_terms and c == 1:
                         flipped = flip(pieces)
                     if places:
-                        b = in_group - 1
+                        b = PLACING_CHUNKS.index(in_group)
                         pre, pos = prepare(k, b)
                     if last_chunk:
                         fold_to_the_end(quarter, NODES // 4, unfolded[1])

@@ -255,7 +255,7 @@ def tile_pgn_b_kernel(
 
             last_chunk = i + 1 == CHUNKS
             scalar_banks = [TURN - 1] * TURNS
-            if places:
+            if k >= 0:
                 scalar_banks[-1] = TURN
             if last_chunk:
                 scalar_banks[-1] = 0

@@ -46,8 +46,7 @@ def tile_pgn_b_kernel(
         tc.tile_pool(name="edges", bufs=6) as edges,
         tc.tile_pool(name="work", bufs=2) as work,
         tc.tile_pool(name="fresh", bufs=3) as fresh,
-        tc.psum_pool(name="banks", bufs=6) as banks,
-        tc.psum_pool(name="side", bufs=2) as side,
+        tc.psum_pool(name="banks", bufs=8) as banks,
     ):
         def load(shape, dtype, source, name):
             tile = held.tile(shape, dtype, name=name)
@@ -144,7 +143,7 @@ def tile_pgn_b_kernel(
             cols = slice(t * NODES, (t + 1) * NODES)
             products = []
             for weights in (w2, w1):
-                product = side.tile([P, NODES], F32, tag="side")
+                product = banks.tile([P, NODES], F32, tag="bank")
                 nc.tensor.matmul(product[:], weights[:, 0, :], node[:, cols], start=True, stop=False)
                 nc.tensor.matmul(product[:], weights[:, 1, :], hid[:, cols], start=False, stop=True)
                 products.append(product)
@@ -169,7 +168,7 @@ def tile_pgn_b_kernel(
             return pieces
 
         def flip(pieces):
-            flipped = side.tile([MASK_ROW, RANGES, P], BF16, tag="side")
+            flipped = banks.tile([MASK_ROW, RANGES, P], BF16, tag="bank")
             for r in range(RANGES):
                 nc.tensor.transpose(flipped[:, r, :], pieces[:, r, :, :].rearrange("p s u -> p (s u)"), ident[:])
             return flipped
@@ -196,7 +195,7 @@ def tile_pgn_b_kernel(
         slots = [held.tile([P, SLOTS], F32, name=f"slots{b}") for b in range(CHANNEL_BLOCKS)]
 
         def fill_bank(chunk, t, c, within):
-            bank = banks.tile([P, BANK_RECEIVERS, NODES], F32)
+            bank = banks.tile([P, BANK_RECEIVERS, NODES], F32, tag="bank")
             nc.tensor.matmul(bank[:], we[:], chunk[:, within : within + BANK_RECEIVERS, :], start=True, stop=False)
             for r in range(RANGES):
                 nc.tensor.matmul(
@@ -224,17 +223,30 @@ def tile_pgn_b_kernel(
             cols = slice(k * PLACED, (k + 1) * PLACED)
             nc.vector.tensor_scalar_max(red[:, cols], red[:, cols], FLOOR)
 
-        def prepare(k, b):
+        def multiply_out(k, b):
             cols = slice(k * PLACED, (k + 1) * PLACED)
             chans = slice(b * P, (b + 1) * P)
-            product = side.tile([P, PLACED], F32, tag="side")
+            product = banks.tile([P, PLACED], F32, tag="bank")
             nc.tensor.matmul(product[:], wo1[:, 0, chans], node[:, cols], start=True, stop=False)
             nc.tensor.matmul(product[:], wo1[:, 1, chans], hid[:, cols], start=False, stop=False)
             nc.tensor.matmul(product[:], wo2[:, chans], red[:, cols], start=False, stop=True)
+            return product
+
+        def prepare(k, b):
+            product = multiply_out(k, b)
             pre = work.tile([P, PLACED], F32)
             nc.scalar.activation(pre[:], product[:], FUNC.Identity, bias=out_bias[:, b : b + 1], scale=1.0)
             pos = work.tile([P, PLACED], F32)
             nc.vector.tensor_single_scalar(pos[:], pre[:], 0.0, op=ALU.is_gt)
+            return pre, pos
+
+        def prepare_on_vector(k, b):
+            product = multiply_out(k, b)
+            bias = out_bias[:, b : b + 1]
+            pre = work.tile([P, PLACED], F32)
+            nc.vector.tensor_scalar_add(pre[:], product[:], bias)
+            pos = work.tile([P, PLACED], F32)
+            nc.vector.tensor_scalar(pos[:], product[:], bias, 0.0, op0=ALU.add, op1=ALU.is_gt)
             return pre, pos
 
         def place(k, b, pre, pos):
@@ -314,7 +326,7 @@ def tile_pgn_b_kernel(
 
         last = N // PLACED - 1
         lay_floor(last)
-        ready = prepare(last, 0)
+        ready = prepare_on_vector(last, 0)
         for b in range(CHANNEL_BLOCKS):
             pre, pos = ready
             if b + 1 < CHANNEL_BLOCKS:

@@ -69,17 +69,17 @@ def tile_pgn_b_kernel(
         load_part(hid, first_nodes, hidden)
         w2 = load([P, 2, P], BF16, W2.rearrange("(h k) m -> k h m", h=2), "w2")
         w1 = load([P, 2, P], BF16, W1.rearrange("(h k) m -> k h m", h=2), "w1")
-        graph_term = load([P, GRAPHS], F32, graph_msg, "graph_term")
-        b1_col = load([P, 1], F32, b1, "b1_col")
-        b2_col = load([P, 1], F32, b2, "b2_col")
-        be_col = load([P, 1], F32, be, "be_col")
-        adj_rows = held.tile([P, CHUNK, NODES], BF16)
-        nc.sync.dma_start(adj_rows[MASK_ROW:P], adj.rearrange("t (c v) u -> (t c) v u", v=CHUNK))
         we = load([P, P], BF16, We, "we")
         first_edges = edge_fts[:, 0, 0:CHUNK, :]
         loaded = [edges.tile([P, CHUNK, NODES], BF16, name="chunk")]
         load_part(loaded[0], slice(0, HEAD), first_edges)
+        adj_rows = held.tile([P, CHUNK, NODES], BF16)
+        nc.sync.dma_start(adj_rows[MASK_ROW:P], adj.rearrange("t (c v) u -> (t c) v u", v=CHUNK))
         load_part(loaded[0], slice(HEAD, CHUNK), first_edges)
+        graph_term = load([P, GRAPHS], F32, graph_msg, "graph_term")
+        b1_col = load([P, 1], F32, b1, "b1_col")
+        b2_col = load([P, 1], F32, b2, "b2_col")
+        be_col = load([P, 1], F32, be, "be_col")
         loaded.append(load_edges(1))
         load_part(node, other_nodes, node_fts)
         load_part(hid, other_nodes, hidden)
@@ -128,7 +128,11 @@ def tile_pgn_b_kernel(
                 pairs[MASK_ROW:P, chunks].bitcast(I32).to_broadcast([CHUNKS, GRAPH_CHUNKS, RANGES * P // 2]),
             )
 
-        write_picks(0)
+        nc.scalar.activation(
+            addend_weights[MASK_ROW:P, 0].rearrange("p c r m -> p c (r m)"),
+            ident[MASK_ROW:P, MASK_ROW : MASK_ROW + GRAPH_CHUNKS].unsqueeze(2).to_broadcast([CHUNKS, GRAPH_CHUNKS, RANGES * P]),
+            FUNC.Identity,
+        )
 
         graph_bias = graph_term
         for name, bias in (("with_b1", b1_col), ("with_b2", b2_col), ("with_be", be_col)):
@@ -183,7 +187,7 @@ def tile_pgn_b_kernel(
             )
 
         write_addend_rows(slice(0, HEAD))
-        keep(flip(take_terms(multiply_by_z(0), 0)), 0)
+        nc.vector.tensor_copy(addend_weights[0:MASK_ROW, 0, 0], flip(take_terms(multiply_by_z(0), 0))[:])
         write_addend_rows(slice(HEAD, CHUNK))
         for c in range(1, GRAPH_CHUNKS):
             nc.vector.tensor_copy(addend_weights[0:MASK_ROW, 0, c], addend_weights[0:MASK_ROW, 0, 0])

@@ -44,6 +44,7 @@ def tile_pgn_b_kernel(
     with (
         tc.tile_pool(name="held", bufs=1) as held,
         tc.tile_pool(name="edges", bufs=6) as edges,
+        tc.tile_pool(name="weights", bufs=2) as weights_pool,
         tc.tile_pool(name="work", bufs=2) as work,
         tc.tile_pool(name="fresh", bufs=3) as fresh,
         tc.psum_pool(name="banks", bufs=8) as banks,
@@ -68,11 +69,11 @@ def tile_pgn_b_kernel(
         load_part(node, first_nodes, node_fts)
         load_part(hid, first_nodes, hidden)
         w2 = load([P, 2, P], BF16, W2.rearrange("(h k) m -> k h m", h=2), "w2")
-        w1 = load([P, 2, P], BF16, W1.rearrange("(h k) m -> k h m", h=2), "w1")
         we = load([P, P], BF16, We, "we")
         first_edges = edge_fts[:, 0, 0:CHUNK, :]
         loaded = [edges.tile([P, CHUNK, NODES], BF16, name="chunk")]
         load_part(loaded[0], slice(0, HEAD), first_edges)
+        w1 = load([P, 2, P], BF16, W1.rearrange("(h k) m -> k h m", h=2), "w1")
         adj_rows = held.tile([P, CHUNK, NODES], BF16)
         nc.sync.dma_start(adj_rows[MASK_ROW:P], adj.rearrange("t (c v) u -> (t c) v u", v=CHUNK))
         load_part(loaded[0], slice(HEAD, CHUNK), first_edges)
@@ -117,19 +118,21 @@ def tile_pgn_b_kernel(
                 op1=ALU.mult,
             )
 
-        addend_weights = held.tile([P, GRAPHS, GRAPH_CHUNKS, RANGES, P], BF16)
         pairs = held.tile([P, CHUNKS, 2], BF16)
         nc.gpsimd.tensor_copy(pairs[MASK_ROW:P], ident[MASK_ROW:P, MASK_ROW:P].unsqueeze(2).to_broadcast([CHUNKS, CHUNKS, 2]))
 
-        def write_picks(t):
+        def new_weights(t):
+            addend_weights = weights_pool.tile([P, GRAPH_CHUNKS, RANGES, P], BF16)
             chunks = slice(t * GRAPH_CHUNKS, (t + 1) * GRAPH_CHUNKS)
             nc.gpsimd.tensor_copy(
-                addend_weights[MASK_ROW:P, t].rearrange("p c r m -> p c (r m)").bitcast(I32),
+                addend_weights[MASK_ROW:P].rearrange("p c r m -> p c (r m)").bitcast(I32),
                 pairs[MASK_ROW:P, chunks].bitcast(I32).to_broadcast([CHUNKS, GRAPH_CHUNKS, RANGES * P // 2]),
             )
+            return addend_weights
 
+        addend_weights = weights_pool.tile([P, GRAPH_CHUNKS, RANGES, P], BF16)
         nc.scalar.activation(
-            addend_weights[MASK_ROW:P, 0].rearrange("p c r m -> p c (r m)"),
+            addend_weights[MASK_ROW:P].rearrange("p c r m -> p c (r m)"),
             ident[MASK_ROW:P, MASK_ROW : MASK_ROW + GRAPH_CHUNKS].unsqueeze(2).to_broadcast([CHUNKS, GRAPH_CHUNKS, RANGES * P]),
             FUNC.Identity,
         )
@@ -139,8 +142,6 @@ def tile_pgn_b_kernel(
             summed = held.tile([P, GRAPHS], F32, name=name)
             nc.scalar.activation(summed[:], graph_bias[:], FUNC.Identity, bias=bias[:, 0:1], scale=1.0)
             graph_bias = summed
-        for t in range(1, GRAPHS):
-            write_picks(t)
         receiver_term = held.tile([P, N], F32)
 
         def multiply_by_z(t):
@@ -177,20 +178,18 @@ def tile_pgn_b_kernel(
                 nc.tensor.transpose(flipped[:, r, :], pieces[:, r, :, :].rearrange("p s u -> p (s u)"), ident[:])
             return flipped
 
-        def keep(flipped, t):
-            nc.scalar.copy(addend_weights[0:MASK_ROW, t, 0], flipped[:])
-
-        def repeat(t):
+        def keep(flipped, weights):
+            nc.scalar.copy(weights[0:MASK_ROW, 0], flipped[:])
             nc.sync.dma_start(
-                addend_weights[0:MASK_ROW, t, 1:GRAPH_CHUNKS],
-                addend_weights[0:MASK_ROW, t, 0:1].to_broadcast([MASK_ROW, GRAPH_CHUNKS - 1, RANGES, P]),
+                weights[0:MASK_ROW, 1:GRAPH_CHUNKS],
+                weights[0:MASK_ROW, 0:1].to_broadcast([MASK_ROW, GRAPH_CHUNKS - 1, RANGES, P]),
             )
 
         write_addend_rows(slice(0, HEAD))
-        nc.vector.tensor_copy(addend_weights[0:MASK_ROW, 0, 0], flip(take_terms(multiply_by_z(0), 0))[:])
+        nc.vector.tensor_copy(addend_weights[0:MASK_ROW, 0], flip(take_terms(multiply_by_z(0), 0))[:])
         write_addend_rows(slice(HEAD, CHUNK))
         for c in range(1, GRAPH_CHUNKS):
-            nc.vector.tensor_copy(addend_weights[0:MASK_ROW, 0, c], addend_weights[0:MASK_ROW, 0, 0])
+            nc.vector.tensor_copy(addend_weights[0:MASK_ROW, c], addend_weights[0:MASK_ROW, 0])
 
         out_bias = held.tile([P, CHANNEL_BLOCKS], F32)
         nc.gpsimd.tensor_add(out_bias[:], bo1_cols[:], bo2_cols[:])
@@ -198,13 +197,13 @@ def tile_pgn_b_kernel(
         red = held.tile([P, N], BF16)
         slots = [held.tile([P, SLOTS], F32, name=f"slots{b}") for b in range(CHANNEL_BLOCKS)]
 
-        def fill_bank(chunk, t, c, within):
+        def fill_bank(chunk, weights, c, within):
             bank = banks.tile([P, BANK_RECEIVERS, NODES], F32, tag="bank")
             nc.tensor.matmul(bank[:], we[:], chunk[:, within : within + BANK_RECEIVERS, :], start=True, stop=False)
             for r in range(RANGES):
                 nc.tensor.matmul(
                     bank[:, :, r * SENDERS : (r + 1) * SENDERS],
-                    addend_weights[:, t, c, r, :],
+                    weights[:, c, r, :],
                     addend_rows[:, r, within : within + BANK_RECEIVERS, :],
                     start=False,
                     stop=(r == RANGES - 1),
@@ -261,6 +260,8 @@ def tile_pgn_b_kernel(
         for i in range(CHUNKS):
             t, c = divmod(i, GRAPH_CHUNKS)
             chunk = loaded[i]
+            if i > 0 and c == 0:
+                addend_weights = next_weights
             if i + LOADS_AHEAD < CHUNKS:
                 loaded.append(load_edges(i + LOADS_AHEAD))
             if i % 2 == 1 and i // 2 < CHANNEL_BLOCKS:
@@ -282,7 +283,7 @@ def tile_pgn_b_kernel(
             for turn in range(TURNS):
                 for s in range(TURN):
                     if s < scalar_banks[turn]:
-                        bank = fill_bank(chunk, t, c, scalar_next)
+                        bank = fill_bank(chunk, addend_weights, c, scalar_next)
                         for v in range(BANK_RECEIVERS):
                             receiver = i * CHUNK + scalar_next + v
                             nc.scalar.activation(
@@ -294,7 +295,7 @@ def tile_pgn_b_kernel(
                             )
                         scalar_next += BANK_RECEIVERS
                     else:
-                        bank = fill_bank(chunk, t, c, vector_next)
+                        bank = fill_bank(chunk, addend_weights, c, vector_next)
                         won = vector_next - scalar_receivers
                         nc.vector.reduce_max(winners[:, won : won + BANK_RECEIVERS], bank[:], axis=INNERMOST)
                         vector_next += BANK_RECEIVERS
@@ -323,8 +324,8 @@ def tile_pgn_b_kernel(
                     if makes_terms and c == 0:
                         pieces = take_terms(products, t + 1)
                     if makes_terms and c == 1:
-                        keep(flipped, t + 1)
-                        repeat(t + 1)
+                        next_weights = new_weights(t + 1)
+                        keep(flipped, next_weights)
                     if places:
                         place(k, b, pre, pos)
 

@@ -81,10 +81,9 @@ def tile_pgn_b_kernel(
         b1_col = load([P, 1], F32, b1, "b1_col")
         b2_col = load([P, 1], F32, b2, "b2_col")
         be_col = load([P, 1], F32, be, "be_col")
-        loaded.append(load_edges(1))
         load_part(node, other_nodes, node_fts)
         load_part(hid, other_nodes, hidden)
-        for i in range(2, LOADS_AHEAD):
+        for i in range(1, LOADS_AHEAD):
             loaded.append(load_edges(i))
         offsets = held.tile([P, N // 16], U16, name="offsets")
         nc.sync.dma_start(offsets[:], offs)
@@ -124,7 +123,7 @@ def tile_pgn_b_kernel(
         def new_weights(t):
             addend_weights = weights_pool.tile([P, GRAPH_CHUNKS, RANGES, P], BF16)
             chunks = slice(t * GRAPH_CHUNKS, (t + 1) * GRAPH_CHUNKS)
-            nc.gpsimd.tensor_copy(
+            nc.vector.tensor_copy(
                 addend_weights[MASK_ROW:P].rearrange("p c r m -> p c (r m)").bitcast(I32),
                 pairs[MASK_ROW:P, chunks].bitcast(I32).to_broadcast([CHUNKS, GRAPH_CHUNKS, RANGES * P // 2]),
             )
@@ -168,7 +167,7 @@ def tile_pgn_b_kernel(
             rest = work.tile([P, RANGES, SENDERS], F32)
             nc.vector.tensor_copy(high, value)
             nc.vector.tensor_sub(rest[:], value, high)
-            nc.vector.tensor_copy(middle, rest[:])
+            nc.vector.tensor_sub(middle, value, high)
             nc.vector.tensor_sub(low, rest[:], middle)
             return pieces
 

@@ -178,7 +178,7 @@ def tile_pgn_b_kernel(
             return flipped
 
         def keep(flipped, weights):
-            nc.scalar.copy(weights[0:MASK_ROW, 0], flipped[:])
+            nc.vector.tensor_copy(weights[0:MASK_ROW, 0], flipped[:])
             nc.sync.dma_start(
                 weights[0:MASK_ROW, 1:GRAPH_CHUNKS],
                 weights[0:MASK_ROW, 0:1].to_broadcast([MASK_ROW, GRAPH_CHUNKS - 1, RANGES, P]),

import concourse.mybir as mybir
from concourse.masks import make_identity

BF16, F32, I32, U16 = mybir.dt.bfloat16, mybir.dt.float32, mybir.dt.int32, mybir.dt.uint16
ALU = mybir.AluOpType
FUNC = mybir.ActivationFunctionType
INNERMOST = mybir.AxisListType.X

P = 128
GRAPHS = 8
NODES = 128
N = GRAPHS * NODES
CHANNELS = 512
CHANNEL_BLOCKS = CHANNELS // P
SLOTS = 2048
BANK = 512
BANK_RECEIVERS = BANK // NODES
SENDERS = 32
RANGES = NODES // SENDERS
PIECES = 3
MASK_ROW = PIECES * SENDERS
CHUNK = NODES // 4
CHUNKS = N // CHUNK
GRAPH_CHUNKS = NODES // CHUNK
HEAD = CHUNK // 4
TURN = 4
TURNS = CHUNK // (BANK_RECEIVERS * TURN)
REDUCED_WIDTH = 8
PLACED = 2 * NODES
LOADS_AHEAD = 4
GROUP_CHUNKS = PLACED // CHUNK
PLACING_CHUNKS = (1, 3, 5, 6)

PENALTY = 2.0**100
FLOOR = -1000000.0

FLOPS = 2 * (P * P * GRAPHS * NODES * NODES + 2 * 2 * P * P * N + 2 * P * CHANNELS * N + P * CHANNELS * N)


def tile_pgn_b_kernel(
    tc, node_fts, hidden, edge_fts, adj, graph_msg, W1, b1, W2, b2, We, be, Wo1, bo1, Wo2, bo2, base, offs, out
):
    nc = tc.nc
    with (
        tc.tile_pool(name="held", bufs=1) as held,
        tc.tile_pool(name="edges", bufs=6) as edges,
        tc.tile_pool(name="weights", bufs=2) as weights_pool,
        tc.tile_pool(name="work", bufs=2) as work,
        tc.tile_pool(name="fresh", bufs=3) as fresh,
        tc.psum_pool(name="banks", bufs=8) as banks,
    ):
        def load(shape, dtype, source, name):
            tile = held.tile(shape, dtype, name=name)
            nc.sync.dma_start(tile[:], source)
            return tile

        def load_part(tile, part, source):
            nc.sync.dma_start(tile[:, part], source[:, part])

        def load_edges(i):
            t, c = divmod(i, GRAPH_CHUNKS)
            chunk = edges.tile([P, CHUNK, NODES], BF16)
            nc.sync.dma_start(chunk[:], edge_fts[:, t, c * CHUNK : (c + 1) * CHUNK, :])
            return chunk

        first_nodes, other_nodes = slice(0, NODES), slice(NODES, N)
        node = held.tile([P, N], BF16)
        hid = held.tile([P, N], BF16)
        load_part(node, first_nodes, node_fts)
        load_part(hid, first_nodes, hidden)
        w2 = load([P, 2, P], BF16, W2.rearrange("(h k) m -> k h m", h=2), "w2")
        we = load([P, P], BF16, We, "we")
        first_edges = edge_fts[:, 0, 0:CHUNK, :]
        loaded = [edges.tile([P, CHUNK, NODES], BF16, name="chunk")]
        load_part(loaded[0], slice(0, HEAD), first_edges)
        w1 = load([P, 2, P], BF16, W1.rearrange("(h k) m -> k h m", h=2), "w1")
        adj_rows = held.tile([P, CHUNK, NODES], BF16)
        nc.sync.dma_start(adj_rows[MASK_ROW:P], adj.rearrange("t (c v) u -> (t c) v u", v=CHUNK))
        load_part(loaded[0], slice(HEAD, CHUNK), first_edges)
        graph_term = load([P, GRAPHS], F32, graph_msg, "graph_term")
        b1_col = load([P, 1], F32, b1, "b1_col")
        b2_col = load([P, 1], F32, b2, "b2_col")
        be_col = load([P, 1], F32, be, "be_col")
        load_part(node, other_nodes, node_fts)
        load_part(hid, other_nodes, hidden)
        for i in range(1, LOADS_AHEAD):
            loaded.append(load_edges(i))
        offsets = held.tile([P, N // 16], U16, name="offsets")
        nc.sync.dma_start(offsets[:], offs)
        wo1 = load([P, 2, CHANNELS], BF16, Wo1.rearrange("(h k) c -> k h c", h=2), "wo1")
        wo2 = load([P, CHANNELS], BF16, Wo2, "wo2")
        with nc.allow_non_contiguous_dma(reason="two bias vectors of 512, one element to a partition"):
            bo1_cols = load([P, CHANNEL_BLOCKS], F32, bo1.rearrange("(b c) one -> c (b one)", c=P), "bo1_cols")
            bo2_cols = load([P, CHANNEL_BLOCKS], F32, bo2.rearrange("(b c) one -> c (b one)", c=P), "bo2_cols")

        ident = held.tile([P, P], BF16)
        make_identity(nc, ident[:])
        same_sender = held.tile([P, SENDERS], BF16)
        with nc.allow_low_precision(reason="each sum is of zeros and at most a single 1"):
            nc.vector.tensor_reduce(
                same_sender[:], ident[:].rearrange("p (s u) -> p u s", u=SENDERS), axis=INNERMOST, op=ALU.add
            )
        addend_rows = held.tile([P, RANGES, CHUNK, SENDERS], BF16)

        def write_addend_rows(part):
            size = part.stop - part.start
            nc.vector.tensor_copy(
                addend_rows[0:MASK_ROW, :, part, :],
                same_sender[0:MASK_ROW].unsqueeze(1).unsqueeze(1).to_broadcast([MASK_ROW, RANGES, size, SENDERS]),
            )
            nc.vector.tensor_scalar(
                addend_rows[MASK_ROW:P, :, part, :].rearrange("p r v u -> p v r u"),
                adj_rows[MASK_ROW:P, part, :].rearrange("p v (r u) -> p v r u", u=SENDERS),
                0.0,
                -PENALTY,
                op0=ALU.is_le,
                op1=ALU.mult,
            )

        pairs = held.tile([P, CHUNKS, 2], BF16)
        nc.gpsimd.tensor_copy(pairs[MASK_ROW:P], ident[MASK_ROW:P, MASK_ROW:P].unsqueeze(2).to_broadcast([CHUNKS, CHUNKS, 2]))

        def new_weights(t):
            addend_weights = weights_pool.tile([P, GRAPH_CHUNKS, RANGES, P], BF16)
            chunks = slice(t * GRAPH_CHUNKS, (t + 1) * GRAPH_CHUNKS)
            nc.vector.tensor_copy(
                addend_weights[MASK_ROW:P].rearrange("p c r m -> p c (r m)").bitcast(I32),
                pairs[MASK_ROW:P, chunks].bitcast(I32).to_broadcast([CHUNKS, GRAPH_CHUNKS, RANGES * P // 2]),
            )
            return addend_weights

        addend_weights = weights_pool.tile([P, GRAPH_CHUNKS, RANGES, P], BF16)
        nc.scalar.activation(
            addend_weights[MASK_ROW:P].rearrange("p c r m -> p c (r m)"),
            ident[MASK_ROW:P, MASK_ROW : MASK_ROW + GRAPH_CHUNKS].unsqueeze(2).to_broadcast([CHUNKS, GRAPH_CHUNKS, RANGES * P]),
            FUNC.Identity,
        )

        graph_bias = graph_term
        for name, bias in (("with_b1", b1_col), ("with_b2", b2_col), ("with_be", be_col)):
            summed = held.tile([P, GRAPHS], F32, name=name)
            nc.scalar.activation(summed[:], graph_bias[:], FUNC.Identity, bias=bias[:, 0:1], scale=1.0)
            graph_bias = summed
        receiver_term = held.tile([P, N], F32)

        def multiply_by_z(t):
            cols = slice(t * NODES, (t + 1) * NODES)
            products = []
            for weights in (w2, w1):
                product = banks.tile([P, NODES], F32, tag="bank")
                nc.tensor.matmul(product[:], weights[:, 0, :], node[:, cols], start=True, stop=False)
                nc.tensor.matmul(product[:], weights[:, 1, :], hid[:, cols], start=False, stop=True)
                products.append(product)
            return products

        def take_terms(products, t):
            nc.scalar.activation(
                receiver_term[:, t * NODES : (t + 1) * NODES],
                products[1][:],
                FUNC.Identity,
                bias=graph_bias[:, t : t + 1],
                scale=1.0,
            )
            value = products[0][:].rearrange("p (r u) -> p r u", u=SENDERS)
            pieces = work.tile([P, RANGES, PIECES, SENDERS], BF16)
            high, middle, low = pieces[:, :, 0, :], pieces[:, :, 1, :], pieces[:, :, 2, :]
            rest = work.tile([P, RANGES, SENDERS], F32)
            nc.vector.tensor_copy(high, value)
            nc.vector.tensor_sub(rest[:], value, high)
            nc.vector.tensor_sub(middle, value, high)
            nc.vector.tensor_sub(low, rest[:], middle)
            return pieces

        def flip(pieces):
            flipped = banks.tile([MASK_ROW, RANGES, P], BF16, tag="bank")
            for r in range(RANGES):
                nc.tensor.transpose(flipped[:, r, :], pieces[:, r, :, :].rearrange("p s u -> p (s u)"), ident[:])
            return flipped

        def keep(flipped, weights):
            nc.vector.tensor_copy(weights[0:MASK_ROW, 0], flipped[:])
            nc.sync.dma_start(
                weights[0:MASK_ROW, 1:GRAPH_CHUNKS],
                weights[0:MASK_ROW, 0:1].to_broadcast([MASK_ROW, GRAPH_CHUNKS - 1, RANGES, P]),
            )

        write_addend_rows(slice(0, HEAD))
        nc.vector.tensor_copy(addend_weights[0:MASK_ROW, 0], flip(take_terms(multiply_by_z(0), 0))[:])
        write_addend_rows(slice(HEAD, CHUNK))
        for c in range(1, GRAPH_CHUNKS):
            nc.vector.tensor_copy(addend_weights[0:MASK_ROW, c], addend_weights[0:MASK_ROW, 0])

        out_bias = held.tile([P, CHANNEL_BLOCKS], F32)
        nc.gpsimd.tensor_add(out_bias[:], bo1_cols[:], bo2_cols[:])

        red = held.tile([P, N], BF16)
        slots = [held.tile([P, SLOTS], F32, name=f"slots{b}") for b in range(CHANNEL_BLOCKS)]

        def fill_bank(chunk, weights, c, within):
            bank = banks.tile([P, BANK_RECEIVERS, NODES], F32, tag="bank")
            nc.tensor.matmul(bank[:], we[:], chunk[:, within : within + BANK_RECEIVERS, :], start=True, stop=False)
            for r in range(RANGES):
                nc.tensor.matmul(
                    bank[:, :, r * SENDERS : (r + 1) * SENDERS],
                    weights[:, c, r, :],
                    addend_rows[:, r, within : within + BANK_RECEIVERS, :],
                    start=False,
                    stop=(r == RANGES - 1),
                )
            return bank

        def fold(wide, width):
            narrow = work.tile([P, wide.shape[1], width], BF16, name=f"narrow{width}")
            nc.vector.tensor_max(narrow[:], wide[:, :, 0:width], wide[:, :, width : 2 * width])
            return narrow[:]

        def fold_to_the_end(wide, width, node_0):
            while width > REDUCED_WIDTH:
                width //= 2
                wide = fold(wide, width)
            with nc.allow_low_precision(reason="a max picks one of its inputs: nothing is accumulated"):
                nc.vector.reduce_max(red[:, node_0 : node_0 + wide.shape[1]], wide, axis=INNERMOST)

        def lay_floor(k):
            cols = slice(k * PLACED, (k + 1) * PLACED)
            nc.vector.tensor_scalar_max(red[:, cols], red[:, cols], FLOOR)

        def multiply_out(k, b):
            cols = slice(k * PLACED, (k + 1) * PLACED)
            chans = slice(b * P, (b + 1) * P)
            product = banks.tile([P, PLACED], F32, tag="bank")
            nc.tensor.matmul(product[:], wo1[:, 0, chans], node[:, cols], start=True, stop=False)
            nc.tensor.matmul(product[:], wo1[:, 1, chans], hid[:, cols], start=False, stop=False)
            nc.tensor.matmul(product[:], wo2[:, chans], red[:, cols], start=False, stop=True)
            return product

        def prepare(k, b):
            product = multiply_out(k, b)
            pre = work.tile([P, PLACED], F32)
            nc.scalar.activation(pre[:], product[:], FUNC.Identity, bias=out_bias[:, b : b + 1], scale=1.0)
            pos = work.tile([P, PLACED], F32)
            nc.vector.tensor_single_scalar(pos[:], pre[:], 0.0, op=ALU.is_gt)
            return pre, pos

        def prepare_on_vector(k, b):
            product = multiply_out(k, b)
            bias = out_bias[:, b : b + 1]
            pre = work.tile([P, PLACED], F32)
            nc.vector.tensor_scalar_add(pre[:], product[:], bias)
            pos = work.tile([P, PLACED], F32)
            nc.vector.tensor_scalar(pos[:], product[:], bias, 0.0, op0=ALU.add, op1=ALU.is_gt)
            return pre, pos

        def place(k, b, pre, pos):
            piece = offsets[:, k * (PLACED // 16) : (k + 1) * (PLACED // 16)]
            nc.vector.tensor_tensor(slots[b][:].indirect(piece), pre[:], pos[:], ALU.mult)

        unfolded = None
        for i in range(CHUNKS):
            t, c = divmod(i, GRAPH_CHUNKS)
            chunk = loaded[i]
            if i > 0 and c == 0:
                addend_weights = next_weights
            if i + LOADS_AHEAD < CHUNKS:
                loaded.append(load_edges(i + LOADS_AHEAD))
            if i % 2 == 1 and i // 2 < CHANNEL_BLOCKS:
                nc.sync.dma_start(slots[i // 2][:], base[(i // 2) * P : (i // 2 + 1) * P, :])
            k, in_group = i // GROUP_CHUNKS - 1, i % GROUP_CHUNKS
            places = k >= 0 and in_group in PLACING_CHUNKS
            makes_terms = t + 1 < GRAPHS

            last_chunk = i + 1 == CHUNKS
            scalar_banks = [TURN - 1] * TURNS
            if k >= 0:
                scalar_banks[-1] = TURN
            if last_chunk:
                scalar_banks[-1] = 0
            scalar_receivers = sum(scalar_banks) * BANK_RECEIVERS
            rounded = fresh.tile([P, scalar_receivers, NODES], BF16)
            winners = fresh.tile([P, CHUNK - scalar_receivers], F32)
            scalar_next, vector_next = 0, scalar_receivers
            for turn in range(TURNS):
                for s in range(TURN):
                    if s < scalar_banks[turn]:
                        bank = fill_bank(chunk, addend_weights, c, scalar_next)
                        for v in range(BANK_RECEIVERS):
                            receiver = i * CHUNK + scalar_next + v
                            nc.scalar.activation(
                                rounded[:, scalar_next + v, :],
                                bank[:, v, :],
                                FUNC.Identity,
                                bias=receiver_term[:, receiver : receiver + 1],
                                scale=1.0,
                            )
                        scalar_next += BANK_RECEIVERS
                    else:
                        bank = fill_bank(chunk, addend_weights, c, vector_next)
                        won = vector_next - scalar_receivers
                        nc.vector.reduce_max(winners[:, won : won + BANK_RECEIVERS], bank[:], axis=INNERMOST)
                        vector_next += BANK_RECEIVERS

                if turn == 0:
                    if unfolded is not None:
                        quarter = fold(fold(unfolded[0], NODES // 2), NODES // 4)
                    if makes_terms and c == 0:
                        products = multiply_by_z(t + 1)
                    if makes_terms and c == 1:
                        flipped = flip(pieces)
                    if places:
                        b = PLACING_CHUNKS.index(in_group)
                        pre, pos = prepare(k, b)
                    if last_chunk:
                        fold_to_the_end(quarter, NODES // 4, unfolded[1])
                        fold_to_the_end(rounded[:], NODES, i * CHUNK)
                else:
                    if unfolded is not None and not last_chunk:
                        fold_to_the_end(quarter, NODES // 4, unfolded[1])
                    if k >= 0 and in_group == 0:
                        lay_floor(k)
                    unfolded = (rounded[:], i * CHUNK)
                    nodes = slice(i * CHUNK + scalar_receivers, (i + 1) * CHUNK)
                    nc.vector.tensor_add(red[:, nodes], winners[:], receiver_term[:, nodes])
                    if makes_terms and c == 0:
                        pieces = take_terms(products, t + 1)
                    if makes_terms and c == 1:
                        next_weights = new_weights(t + 1)
                        keep(flipped, next_weights)
                    if places:
                        place(k, b, pre, pos)

        last = N // PLACED - 1
        lay_floor(last)
        ready = prepare_on_vector(last, 0)
        for b in range(CHANNEL_BLOCKS):
            pre, pos = ready
            if b + 1 < CHANNEL_BLOCKS:
                ready = prepare(last, b + 1)
            place(last, b, pre, pos)
            nc.sync.dma_start(out[b * P : (b + 1) * P, :], slots[b][:])
